import numpy as np
import ml_dtypes


def mxq(x, axis, fmt="e4m3"):
    dtype, down = {"e4m3": (ml_dtypes.float8_e4m3fn, 7), "e5m2": (ml_dtypes.float8_e5m2, 14)}[fmt]
    v = np.moveaxis(np.asarray(x, np.float32).astype(ml_dtypes.bfloat16).astype(np.float64), axis, -1)
    blocks = v.reshape(v.shape[:-1] + (-1, 32))
    amax = np.abs(blocks).max(-1, keepdims=True)
    byte = np.maximum(np.where(amax > 0, np.frexp(amax)[1] - 1 + 127, 0) - down, 1)
    scale = np.exp2(byte - 127.0)
    codes = (blocks / scale).astype(np.float32).astype(dtype).astype(np.float64)
    return np.moveaxis((codes * scale).reshape(v.shape), -1, axis)


WIDE = False


def mx_kscale(k):
    if not WIDE:
        return np.ones(k)
    levels = np.array([10, -10, 5, -5, 0])
    a = np.random.permutation(np.resize(levels, k // 512 * 4)).reshape(k // 512, 4)
    idx = np.arange(k)
    return np.exp2(a[idx // 512, idx % 128 // 32])


BF16 = ml_dtypes.bfloat16


def bf(x):
    return np.asarray(x, np.float32).astype(BF16)


def f64(x):
    return np.asarray(x).astype(np.float64)


B, L, D, H, KV, HD, QB = 1, 1024, 1024, 4, 2, 256, 512
EPS_RMS = 1e-6
EPS_NORM = 1e-12


def rmsnorm(x, w):
    var = np.mean(np.square(x), axis=-1, keepdims=True)
    return x * (1.0 / np.sqrt(var + EPS_RMS)) * w


def l2norm(x):
    n = np.sqrt(np.sum(np.square(x), axis=-1, keepdims=True))
    return x / np.maximum(n, EPS_NORM)


def heads(y, n):
    return y.reshape(B, L, n, HD).transpose(0, 2, 1, 3)


def setup_inputs():
    s = mx_kscale(D)
    c = 1.0 / np.sqrt(D)
    return {"x": bf(np.random.standard_normal((B, L, D)) * np.exp(0.5 * np.random.standard_normal((B, L, 1)))),
            "norm_w": bf((1.0 + 0.1 * np.random.standard_normal(D)) * s),
            "Wq": bf(np.random.standard_normal((D, H * HD)) * c / s[:, None]),
            "Wk": bf(np.random.standard_normal((D, KV * HD)) * c / s[:, None]),
            "Wv": bf(np.random.standard_normal((D, KV * HD)) * c / s[:, None])}


def reference(x, norm_w, Wq, Wk, Wv):
    h = mxq(rmsnorm(f64(x), f64(norm_w)), 2, "e4m3")
    q = heads(h @ mxq(f64(Wq), 0, "e4m3"), H)
    k = heads(h @ mxq(f64(Wk), 0, "e4m3"), KV)
    v = heads(h @ mxq(f64(Wv), 0, "e4m3"), KV)
    return l2norm(q), l2norm(k), v

@@ -1,0 +1,197 @@
+from contextlib import ExitStack
+
+import concourse.mybir as mybir
+from concourse.masks import make_identity
+
+FLOPS = 2 * 1024 * 1024 * 2048
+
+BF16 = mybir.dt.bfloat16
+F32 = mybir.dt.float32
+U32 = mybir.dt.uint32
+U8 = mybir.dt.uint8
+FP8X4 = mybir.dt.float8_e4m3fn_x4
+ACT = mybir.ActivationFunctionType
+ALU = mybir.AluOpType
+
+P = 128
+L = 1024
+D = 1024
+HD = 256
+MT = L // P
+NB = 4
+NBW = 512
+G = 2
+EPS_RMS = 1e-6
+EPS_NORM = 1e-12
+
+
+def tile_sharedglobalattention_pa_kernel(tc, x, norm_w, Wq, Wk, Wv, out_0, out_1, out_2):
+    nc = tc.nc
+    with ExitStack() as ctx:
+        keep = ctx.enter_context(tc.tile_pool(name="keep", bufs=1))
+        stage_pool = ctx.enter_context(tc.tile_pool(name="stage", bufs=1))
+        work = ctx.enter_context(tc.tile_pool(name="work", bufs=3))
+        small = ctx.enter_context(tc.tile_pool(name="small", bufs=4))
+        psum = ctx.enter_context(tc.psum_pool(name="psum", bufs=7))
+        psum_w = ctx.enter_context(tc.psum_pool(name="psum_w", bufs=1))
+
+        eps_t = keep.tile([P, 1], F32, name="eps_t")
+        nc.vector.memset(eps_t[:], EPS_RMS)
+        warm = keep.tile([P, 1], F32, name="warm")
+        nc.scalar.activation(out=warm[:], in_=eps_t[:], func=ACT.Sqrt)
+        nw_row = keep.tile([P, D], BF16, name="nw_row")
+        nc.vector.memset(nw_row[:], 0.0)
+        ones = keep.tile([P, P], BF16, name="ones")
+        nc.vector.memset(ones[:], 1.0)
+        ident = keep.tile([P, P], BF16, name="ident")
+        make_identity(nc, ident[:])
+
+        nw_in = keep.tile([1, D], BF16, name="nw_in")
+        nc.sync.dma_start(out=nw_in[:], in_=norm_w.rearrange("(o k) -> o k", o=1))
+        x_sb = keep.tile([P, MT, D], BF16, name="x_sb")
+        x_view = x.rearrange("b (p m) k -> p (b m) k", m=MT)
+        w_src = [
+            Wq[:, 0:NBW].rearrange("(c p) n -> p c n", p=P),
+            Wq[:, NBW : 2 * NBW].rearrange("(c p) n -> p c n", p=P),
+            Wk.rearrange("(c p) n -> p c n", p=P),
+            Wv.rearrange("(c p) n -> p c n", p=P),
+        ]
+        w_raw = [keep.tile([P, 4 * G, NBW], BF16, name="w_raw%d" % nb) for nb in range(NB)]
+
+        def load_x(m0, m1):
+            nc.sync.dma_start(out=x_sb[:, m0:m1, :], in_=x_view[:, m0:m1, :])
+
+        def load_w(nb, g):
+            rows = slice(4 * g, 4 * g + 4)
+            nc.sync.dma_start(out=w_raw[nb][:, rows, :], in_=w_src[nb][:, rows, :])
+
+        load_w(0, 0)
+        load_x(0, 1)
+        load_x(1, 2)
+        load_w(0, 1)
+        load_x(2, 4)
+        load_w(3, 0)
+        load_w(3, 1)
+        load_x(4, 6)
+        load_x(6, 8)
+        load_w(1, 0)
+        load_w(1, 1)
+        load_w(2, 0)
+        load_w(2, 1)
+
+        nc.vector.tensor_copy(out=nw_row[0:1, :], in_=nw_in[:])
+        wb = psum_w.tile([P, D], BF16, name="wb")
+        for half in range(2):
+            cols = slice(half * 512, (half + 1) * 512)
+            nc.tensor.matmul(wb[:, cols], lhsT=ones[:], rhs=nw_row[:, cols], start=True, stop=True)
+
+        h_codes = keep.tile([P, MT, G * P], U32, name="h_codes", align_bytes=64)
+        h_scales = keep.tile([P, MT, G * P], U8, name="h_scales", align_bytes=64)
+        w_codes = keep.tile([P, NB, G, NBW], U32, name="w_codes", align_bytes=64)
+        w_scales = keep.tile([P, NB, G, NBW], U8, name="w_scales", align_bytes=64)
+
+        def prep_w(nb):
+            grouped = []
+            for g in range(G):
+                wg = work.tile([P, NBW, 4], BF16, name="wg", tag="wg", bufs=4, align_bytes=64)
+                nc.vector.tensor_copy(
+                    out=wg[:].rearrange("p (c i) t -> p c t i", i=4),
+                    in_=w_raw[nb][:, 4 * g : 4 * g + 4, :].rearrange("p t (c i) -> p c t i", i=4),
+                )
+                grouped.append(wg)
+            for g in range(G):
+                nc.vector.quantize_mx(
+                    out=w_codes[:, nb, g, :].bitcast(FP8X4),
+                    scales=w_scales[:, nb, g, :],
+                    in_=grouped[g][:].rearrange("p n t -> p (n t)"),
+                )
+
+        def stats(m):
+            junk = work.tile([P, D], BF16, name="junk", tag="junk", bufs=2)
+            ss = small.tile([P, 1], F32, name="ss", tag="ss")
+            nc.scalar.activation(out=junk[:], in_=x_sb[:, m, :], func=ACT.Square, accum_out=ss[:])
+            sd = small.tile([P, 1], F32, name="sd", tag="sd")
+            nc.scalar.activation(out=sd[:], in_=ss[:], func=ACT.Sqrt, scale=1.0 / D, bias=eps_t[:])
+            rstd = small.tile([P, 1], F32, name="rstd", tag="rstd")
+            nc.vector.reciprocal(out=rstd[:], in_=sd[:])
+            return rstd
+
+        def prep_h(m, rstd):
+            h_sb = work.tile([P, D], BF16, name="h_sb", tag="h_sb")
+            nc.vector.scalar_tensor_tensor(
+                out=h_sb[:], in0=x_sb[:, m, :], scalar=rstd[:, 0:1], in1=wb[:], op0=ALU.mult, op1=ALU.mult
+            )
+            tp = psum.tile([P, 4 * G, P], BF16, name="tp", tag="bank")
+            for c in range(4 * G):
+                nc.tensor.transpose(tp[:, c, :], h_sb[:, c * P : (c + 1) * P], ident[:])
+            hg = work.tile([P, G, P, 4], BF16, name="hg", tag="hg", align_bytes=64)
+            nc.scalar.copy(out=hg[:], in_=tp[:].rearrange("p (g t) r -> p g r t", g=G))
+            nc.vector.quantize_mx(
+                out=h_codes[:, m, :].bitcast(FP8X4),
+                scales=h_scales[:, m, :],
+                in_=hg[:].rearrange("p g r t -> p (g r t)"),
+            )
+
+        def project(m, nb):
+            acc = psum.tile([P, NBW], F32, name="acc", tag="bank")
+            for g in range(G):
+                nc.tensor.matmul_mx(
+                    out=acc[:],
+                    lhsT=h_codes[:, m, g * P : (g + 1) * P].bitcast(FP8X4),
+                    lhsT_scale=h_scales[:, m, g * P : (g + 1) * P],
+                    rhs=w_codes[:, nb, g, :].bitcast(FP8X4),
+                    rhs_scale=w_scales[:, nb, g, :],
+                    start=(g == 0),
+                    stop=(g == G - 1),
+                )
+            return acc
+
+        out_views = [
+            out_0.rearrange("b h (p m) d -> p (b h) m d", m=MT)[:, 0:2],
+            out_0.rearrange("b h (p m) d -> p (b h) m d", m=MT)[:, 2:4],
+            out_1.rearrange("b h (p m) d -> p (b h) m d", m=MT),
+            out_2.rearrange("b h (p m) d -> p (b h) m d", m=MT),
+        ]
+
+        def out_pair(j, nb):
+            st = stage_pool.tile([P, 2, 2, HD], F32, name="st_%d_%d" % (nb, j))
+            accs = [project(2 * j + i, nb) for i in range(2)]
+            if nb < 3:
+                ss4 = small.tile([P, 4], F32, name="ss4", tag="ss4")
+                for i in range(2):
+                    for hh in range(2):
+                        jq = work.tile([P, HD], BF16, name="jq", tag="jq", bufs=2)
+                        nc.scalar.activation(
+                            out=jq[:],
+                            in_=accs[i][:, hh * HD : (hh + 1) * HD],
+                            func=ACT.Square,
+                            accum_out=ss4[:, 2 * i + hh : 2 * i + hh + 1],
+                        )
+                nr = small.tile([P, 4], F32, name="nr", tag="nr")
+                nc.scalar.activation(out=nr[:], in_=ss4[:], func=ACT.Sqrt)
+                nm = small.tile([P, 4], F32, name="nm", tag="nm")
+                nc.vector.tensor_scalar_max(out=nm[:], in0=nr[:], scalar1=EPS_NORM)
+                rn = small.tile([P, 4], F32, name="rn", tag="rn")
+                nc.vector.reciprocal(out=rn[:], in_=nm[:])
+                for i in range(2):
+                    nc.vector.tensor_tensor(
+                        out=st[:, :, i, :],
+                        in0=accs[i][:].rearrange("p (h d) -> p h d", h=2),
+                        in1=rn[:, 2 * i : 2 * i + 2].unsqueeze(2).to_broadcast([P, 2, HD]),
+                        op=ALU.mult,
+                    )
+            else:
+                nc.scalar.copy(out=st[:, :, 0, :], in_=accs[0][:].rearrange("p (h d) -> p h d", h=2))
+                nc.scalar.copy(out=st[:, :, 1, :], in_=accs[1][:].rearrange("p (h d) -> p h d", h=2))
+            nc.sync.dma_start(out=out_views[nb][:, :, 2 * j : 2 * j + 2, :], in_=st[:])
+
+        prep_w(0)
+        for j in range(MT // 2):
+            rs = [stats(2 * j + i) for i in range(2)]
+            for i in range(2):
+                prep_h(2 * j + i, rs[i])
+            out_pair(j, 0)
+        for nb in (3, 1, 2):
+            prep_w(nb)
+            for j in range(MT // 2):
+                out_pair(j, nb)

@@ -24,31 +24,71 @@ G = 2
 EPS_RMS = 1e-6
 EPS_NORM = 1e-12
 
+ORDER = [
+    ("memset",), ("ld_nw",), ("ld_w", 0, 0), ("ld_x", 0, 1), ("ld_x", 1, 2), ("ld_w", 0, 1),
+    ("ld_x", 2, 4), ("ld_w", 3, 0), ("ld_w", 3, 1), ("ld_x", 4, 6), ("ld_x", 6, 8), ("ld_w", 1, 0),
+    ("ld_w", 1, 1), ("ld_w", 2, 0), ("ld_w", 2, 1), ("nwcopy",), ("nwmm",), ("R", 0, 0),
+    ("sq", 0), ("sd", 0), ("sq", 1), ("rs", 0), ("stt", 0), ("sd", 1),
+    ("R", 0, 1), ("tp", 0), ("sq", 2), ("QW", 0), ("co", 0), ("rs", 1),
+    ("stt", 1), ("sd", 2), ("sq", 3), ("qh", 0, 1), ("tp", 1), ("sd", 3),
+    ("rs", 2), ("sq", 4), ("rs", 3), ("stt", 2), ("mm", 0, 0), ("co", 1),
+    ("stt", 3), ("tp", 2), ("s2", 0, 0, 0), ("qh", 1, 2), ("s2", 0, 0, 1), ("tp", 3),
+    ("R", 3, 0), ("co", 2), ("mm", 1, 0), ("R", 3, 1), ("co", 3), ("s2", 1, 0, 0),
+    ("QW", 3), ("s2", 1, 0, 1), ("sr", 0, 0), ("sd", 4), ("sq", 5), ("rc", 0, 0),
+    ("mm", 0, 3), ("sc", 0, 0), ("mm", 1, 3), ("sc", 1, 0), ("sd", 5), ("sq", 6),
+    ("qh", 2, 4), ("st", 0, 0, 0, 2), ("rs", 4), ("mm", 2, 0), ("sd", 6), ("rs", 5),
+    ("sq", 7), ("stt", 4), ("mm", 3, 0), ("mm", 2, 3), ("s2", 2, 0, 0), ("stt", 5),
+    ("s2", 2, 0, 1), ("tp", 4), ("s2", 3, 0, 0), ("s2", 3, 0, 1), ("rs", 6), ("stt", 6),
+    ("tp", 5), ("sr", 1, 0), ("co", 4), ("rc", 1, 0), ("co", 5), ("tp", 6),
+    ("sc", 2, 0), ("sc", 3, 0), ("mm", 3, 3), ("sd", 7), ("co", 6), ("qh", 4, 6),
+    ("st", 1, 0, 0, 2), ("rs", 7), ("mm", 4, 0), ("stt", 7), ("vc", 0), ("mm", 5, 0),
+    ("s2", 4, 0, 0), ("mm", 4, 3), ("R", 1, 0), ("s2", 4, 0, 1), ("s2", 5, 0, 0), ("tp", 7),
+    ("s2", 5, 0, 1), ("sr", 2, 0), ("R", 1, 1), ("vc", 1), ("mm", 5, 3), ("co", 7),
+    ("st", 0, 3, 0, 2), ("rc", 2, 0), ("sc", 4, 0), ("vc", 2), ("sc", 5, 0), ("vc", 3),
+    ("qh", 6, 8), ("st", 2, 0, 0, 2), ("vc", 4), ("st", 1, 3, 0, 2), ("QW", 1), ("mm", 6, 0),
+    ("vc", 5), ("mm", 7, 0), ("s2", 6, 0, 0), ("st", 2, 3, 0, 2), ("s2", 6, 0, 1), ("R", 2, 0),
+    ("mm", 6, 3), ("s2", 7, 0, 0), ("mm", 7, 3), ("s2", 7, 0, 1), ("sr", 3, 0), ("R", 2, 1),
+    ("mm", 0, 1), ("vc", 6), ("mm", 1, 1), ("vc", 7), ("mm", 2, 1), ("rc", 3, 0),
+    ("s2", 0, 1, 0), ("sc", 6, 0), ("st", 3, 3, 0, 2), ("s2", 0, 1, 1), ("mm", 3, 1), ("s2", 1, 1, 0),
+    ("sc", 7, 0), ("mm", 4, 1), ("s2", 1, 1, 1), ("QW", 2), ("sr", 0, 1), ("st", 3, 0, 0, 2),
+    ("s2", 2, 1, 0), ("mm", 5, 1), ("s2", 2, 1, 1), ("mm", 6, 1), ("s2", 3, 1, 0), ("rc", 0, 1),
+    ("s2", 3, 1, 1), ("sc", 0, 1), ("mm", 7, 1), ("sr", 1, 1), ("s2", 4, 1, 0), ("sc", 1, 1),
+    ("mm", 0, 2), ("s2", 4, 1, 1), ("s2", 5, 1, 0), ("rc", 1, 1), ("mm", 1, 2), ("st", 0, 1, 0, 2),
+    ("sc", 2, 1), ("s2", 5, 1, 1), ("sr", 2, 1), ("s2", 6, 1, 0), ("sc", 3, 1), ("mm", 2, 2),
+    ("s2", 6, 1, 1), ("rc", 2, 1), ("mm", 3, 2), ("s2", 7, 1, 0), ("st", 1, 1, 0, 2), ("sc", 4, 1),
+    ("s2", 7, 1, 1), ("sc", 5, 1), ("mm", 4, 2), ("sr", 3, 1), ("s2", 0, 2, 0), ("s2", 0, 2, 1),
+    ("rc", 3, 1), ("mm", 5, 2), ("st", 2, 1, 0, 2), ("sc", 6, 1), ("s2", 1, 2, 0), ("s2", 1, 2, 1),
+    ("sc", 7, 1), ("mm", 6, 2), ("sr", 0, 2), ("s2", 2, 2, 0), ("rc", 0, 2), ("mm", 7, 2),
+    ("s2", 2, 2, 1), ("st", 3, 1, 0, 2), ("sc", 0, 2), ("s2", 3, 2, 0), ("sc", 1, 2), ("s2", 3, 2, 1),
+    ("sr", 1, 2), ("s2", 4, 2, 0), ("rc", 1, 2), ("st", 0, 2, 0, 2), ("sc", 2, 2), ("s2", 4, 2, 1),
+    ("s2", 5, 2, 0), ("sc", 3, 2), ("s2", 5, 2, 1), ("sr", 2, 2), ("s2", 6, 2, 0), ("st", 1, 2, 0, 2),
+    ("rc", 2, 2), ("sc", 4, 2), ("s2", 6, 2, 1), ("s2", 7, 2, 0), ("sc", 5, 2), ("s2", 7, 2, 1),
+    ("sr", 3, 2), ("st", 2, 2, 0, 2), ("rc", 3, 2), ("sc", 6, 2), ("sc", 7, 2), ("st", 3, 2, 0, 1),
+    ("st", 3, 2, 1, 2),
+]
+
 
 def tile_sharedglobalattention_pa_kernel(tc, x, norm_w, Wq, Wk, Wv, out_0, out_1, out_2):
     nc = tc.nc
     with ExitStack() as ctx:
         keep = ctx.enter_context(tc.tile_pool(name="keep", bufs=1))
-        stage_pool = ctx.enter_context(tc.tile_pool(name="stage", bufs=1))
-        work = ctx.enter_context(tc.tile_pool(name="work", bufs=3))
-        small = ctx.enter_context(tc.tile_pool(name="small", bufs=4))
-        psum = ctx.enter_context(tc.psum_pool(name="psum", bufs=7))
-        psum_w = ctx.enter_context(tc.psum_pool(name="psum_w", bufs=1))
+        psum = ctx.enter_context(tc.psum_pool(name="psum", bufs=8))
+        ctx.enter_context(tc.manual_schedule())
 
         eps_t = keep.tile([P, 1], F32, name="eps_t")
-        nc.vector.memset(eps_t[:], EPS_RMS)
         warm = keep.tile([P, 1], F32, name="warm")
-        nc.scalar.activation(out=warm[:], in_=eps_t[:], func=ACT.Sqrt)
-        nw_row = keep.tile([P, D], BF16, name="nw_row")
-        nc.vector.memset(nw_row[:], 0.0)
-        ones = keep.tile([P, P], BF16, name="ones")
-        nc.vector.memset(ones[:], 1.0)
-        ident = keep.tile([P, P], BF16, name="ident")
-        make_identity(nc, ident[:])
-
         nw_in = keep.tile([1, D], BF16, name="nw_in")
-        nc.sync.dma_start(out=nw_in[:], in_=norm_w.rearrange("(o k) -> o k", o=1))
+        nw_row = keep.tile([P, D], BF16, name="nw_row")
+        ones = keep.tile([P, P], BF16, name="ones")
+        ident = keep.tile([P, P], BF16, name="ident")
         x_sb = keep.tile([P, MT, D], BF16, name="x_sb")
+        w_raw = [keep.tile([P, 4 * G, NBW], BF16, name="w_raw%d" % nb) for nb in range(NB)]
+        h_codes = keep.tile([P, MT, G * P], U32, name="h_codes", align_bytes=64)
+        h_scales = keep.tile([P, MT, G * P], U8, name="h_scales", align_bytes=64)
+        w_codes = keep.tile([P, NB, G * NBW], U32, name="w_codes", align_bytes=64)
+        w_scales = keep.tile([P, NB, G * NBW], U8, name="w_scales", align_bytes=64)
+        junk = keep.tile([P, D], BF16, name="junk")
+
         x_view = x.rearrange("b (p m) k -> p (b m) k", m=MT)
         w_src = [
             Wq[:, 0:NBW].rearrange("(c p) n -> p c n", p=P),
@@ -56,142 +96,166 @@ def tile_sharedglobalattention_pa_kernel(tc, x, norm_w, Wq, Wk, Wv, out_0, out_1
             Wk.rearrange("(c p) n -> p c n", p=P),
             Wv.rearrange("(c p) n -> p c n", p=P),
         ]
-        w_raw = [keep.tile([P, 4 * G, NBW], BF16, name="w_raw%d" % nb) for nb in range(NB)]
-
-        def load_x(m0, m1):
-            nc.sync.dma_start(out=x_sb[:, m0:m1, :], in_=x_view[:, m0:m1, :])
-
-        def load_w(nb, g):
-            rows = slice(4 * g, 4 * g + 4)
-            nc.sync.dma_start(out=w_raw[nb][:, rows, :], in_=w_src[nb][:, rows, :])
-
-        load_w(0, 0)
-        load_x(0, 1)
-        load_x(1, 2)
-        load_w(0, 1)
-        load_x(2, 4)
-        load_w(3, 0)
-        load_w(3, 1)
-        load_x(4, 6)
-        load_x(6, 8)
-        load_w(1, 0)
-        load_w(1, 1)
-        load_w(2, 0)
-        load_w(2, 1)
-
-        nc.vector.tensor_copy(out=nw_row[0:1, :], in_=nw_in[:])
-        wb = psum_w.tile([P, D], BF16, name="wb")
-        for half in range(2):
-            cols = slice(half * 512, (half + 1) * 512)
-            nc.tensor.matmul(wb[:, cols], lhsT=ones[:], rhs=nw_row[:, cols], start=True, stop=True)
-
-        h_codes = keep.tile([P, MT, G * P], U32, name="h_codes", align_bytes=64)
-        h_scales = keep.tile([P, MT, G * P], U8, name="h_scales", align_bytes=64)
-        w_codes = keep.tile([P, NB, G, NBW], U32, name="w_codes", align_bytes=64)
-        w_scales = keep.tile([P, NB, G, NBW], U8, name="w_scales", align_bytes=64)
-
-        def prep_w(nb):
-            grouped = []
-            for g in range(G):
-                wg = work.tile([P, NBW, 4], BF16, name="wg", tag="wg", bufs=4, align_bytes=64)
-                nc.vector.tensor_copy(
-                    out=wg[:].rearrange("p (c i) t -> p c t i", i=4),
-                    in_=w_raw[nb][:, 4 * g : 4 * g + 4, :].rearrange("p t (c i) -> p c t i", i=4),
-                )
-                grouped.append(wg)
-            for g in range(G):
-                nc.vector.quantize_mx(
-                    out=w_codes[:, nb, g, :].bitcast(FP8X4),
-                    scales=w_scales[:, nb, g, :],
-                    in_=grouped[g][:].rearrange("p n t -> p (n t)"),
-                )
-
-        def stats(m):
-            junk = work.tile([P, D], BF16, name="junk", tag="junk", bufs=2)
-            ss = small.tile([P, 1], F32, name="ss", tag="ss")
-            nc.scalar.activation(out=junk[:], in_=x_sb[:, m, :], func=ACT.Square, accum_out=ss[:])
-            sd = small.tile([P, 1], F32, name="sd", tag="sd")
-            nc.scalar.activation(out=sd[:], in_=ss[:], func=ACT.Sqrt, scale=1.0 / D, bias=eps_t[:])
-            rstd = small.tile([P, 1], F32, name="rstd", tag="rstd")
-            nc.vector.reciprocal(out=rstd[:], in_=sd[:])
-            return rstd
-
-        def prep_h(m, rstd):
-            h_sb = work.tile([P, D], BF16, name="h_sb", tag="h_sb")
-            nc.vector.scalar_tensor_tensor(
-                out=h_sb[:], in0=x_sb[:, m, :], scalar=rstd[:, 0:1], in1=wb[:], op0=ALU.mult, op1=ALU.mult
-            )
-            tp = psum.tile([P, 4 * G, P], BF16, name="tp", tag="bank")
-            for c in range(4 * G):
-                nc.tensor.transpose(tp[:, c, :], h_sb[:, c * P : (c + 1) * P], ident[:])
-            hg = work.tile([P, G, P, 4], BF16, name="hg", tag="hg", align_bytes=64)
-            nc.scalar.copy(out=hg[:], in_=tp[:].rearrange("p (g t) r -> p g r t", g=G))
-            nc.vector.quantize_mx(
-                out=h_codes[:, m, :].bitcast(FP8X4),
-                scales=h_scales[:, m, :],
-                in_=hg[:].rearrange("p g r t -> p (g r t)"),
-            )
-
-        def project(m, nb):
-            acc = psum.tile([P, NBW], F32, name="acc", tag="bank")
-            for g in range(G):
-                nc.tensor.matmul_mx(
-                    out=acc[:],
-                    lhsT=h_codes[:, m, g * P : (g + 1) * P].bitcast(FP8X4),
-                    lhsT_scale=h_scales[:, m, g * P : (g + 1) * P],
-                    rhs=w_codes[:, nb, g, :].bitcast(FP8X4),
-                    rhs_scale=w_scales[:, nb, g, :],
-                    start=(g == 0),
-                    stop=(g == G - 1),
-                )
-            return acc
-
         out_views = [
             out_0.rearrange("b h (p m) d -> p (b h) m d", m=MT)[:, 0:2],
             out_0.rearrange("b h (p m) d -> p (b h) m d", m=MT)[:, 2:4],
             out_1.rearrange("b h (p m) d -> p (b h) m d", m=MT),
             out_2.rearrange("b h (p m) d -> p (b h) m d", m=MT),
         ]
+        t = {}
 
-        def out_pair(j, nb):
-            st = stage_pool.tile([P, 2, 2, HD], F32, name="st_%d_%d" % (nb, j))
-            accs = [project(2 * j + i, nb) for i in range(2)]
-            if nb < 3:
-                ss4 = small.tile([P, 4], F32, name="ss4", tag="ss4")
-                for i in range(2):
-                    for hh in range(2):
-                        jq = work.tile([P, HD], BF16, name="jq", tag="jq", bufs=2)
-                        nc.scalar.activation(
-                            out=jq[:],
-                            in_=accs[i][:, hh * HD : (hh + 1) * HD],
-                            func=ACT.Square,
-                            accum_out=ss4[:, 2 * i + hh : 2 * i + hh + 1],
-                        )
-                nr = small.tile([P, 4], F32, name="nr", tag="nr")
-                nc.scalar.activation(out=nr[:], in_=ss4[:], func=ACT.Sqrt)
-                nm = small.tile([P, 4], F32, name="nm", tag="nm")
-                nc.vector.tensor_scalar_max(out=nm[:], in0=nr[:], scalar1=EPS_NORM)
-                rn = small.tile([P, 4], F32, name="rn", tag="rn")
-                nc.vector.reciprocal(out=rn[:], in_=nm[:])
-                for i in range(2):
-                    nc.vector.tensor_tensor(
-                        out=st[:, :, i, :],
-                        in0=accs[i][:].rearrange("p (h d) -> p h d", h=2),
-                        in1=rn[:, 2 * i : 2 * i + 2].unsqueeze(2).to_broadcast([P, 2, HD]),
-                        op=ALU.mult,
-                    )
-            else:
-                nc.scalar.copy(out=st[:, :, 0, :], in_=accs[0][:].rearrange("p (h d) -> p h d", h=2))
-                nc.scalar.copy(out=st[:, :, 1, :], in_=accs[1][:].rearrange("p (h d) -> p h d", h=2))
-            nc.sync.dma_start(out=out_views[nb][:, :, 2 * j : 2 * j + 2, :], in_=st[:])
+        def op_memset():
+            nc.vector.memset(eps_t[:], EPS_RMS)
+            nc.scalar.activation(out=warm[:], in_=eps_t[:], func=ACT.Sqrt)
+            nc.vector.memset(nw_row[:], 0.0)
+            nc.vector.memset(ones[:], 1.0)
+            make_identity(nc, ident[:])
 
-        prep_w(0)
-        for j in range(MT // 2):
-            rs = [stats(2 * j + i) for i in range(2)]
-            for i in range(2):
-                prep_h(2 * j + i, rs[i])
-            out_pair(j, 0)
-        for nb in (3, 1, 2):
-            prep_w(nb)
-            for j in range(MT // 2):
-                out_pair(j, nb)
+        def op_ld_nw():
+            nc.sync.dma_start(out=nw_in[:], in_=norm_w.rearrange("(o k) -> o k", o=1))
+
+        def op_ld_x(m0, m1):
+            nc.sync.dma_start(out=x_sb[:, m0:m1, :], in_=x_view[:, m0:m1, :])
+
+        def op_ld_w(nb, g):
+            rows = slice(4 * g, 4 * g + 4)
+            nc.sync.dma_start(out=w_raw[nb][:, rows, :], in_=w_src[nb][:, rows, :])
+
+        def op_nwcopy():
+            nc.vector.tensor_copy(out=nw_row[0:1, :], in_=nw_in[:])
+
+        def op_nwmm():
+            t["wb"] = psum.tile([P, D], BF16, name="wb", tag="bank")
+            for half in range(2):
+                cols = slice(half * 512, (half + 1) * 512)
+                nc.tensor.matmul(t["wb"][:, cols], lhsT=ones[:], rhs=nw_row[:, cols], start=True, stop=True)
+
+        def op_R(nb, g):
+            if ("wg", nb) not in t:
+                t[("wg", nb)] = keep.tile([P, G, NBW, 4], BF16, name="wg_%d" % nb, align_bytes=64)
+            nc.vector.tensor_copy(
+                out=t[("wg", nb)][:, g].rearrange("p (c i) t -> p c t i", i=4),
+                in_=w_raw[nb][:, 4 * g : 4 * g + 4, :].rearrange("p t (c i) -> p c t i", i=4),
+            )
+
+        def op_QW(nb):
+            nc.vector.quantize_mx(
+                out=w_codes[:, nb, :].bitcast(FP8X4),
+                scales=w_scales[:, nb, :],
+                in_=t[("wg", nb)][:].rearrange("p g n t -> p (g n t)"),
+            )
+
+        def op_sq(m):
+            t[("ss", m)] = keep.tile([P, 1], F32, name="ss_%d" % m)
+            nc.scalar.activation(out=junk[:], in_=x_sb[:, m, :], func=ACT.Square, accum_out=t[("ss", m)][:])
+
+        def op_sd(m):
+            t[("sd", m)] = keep.tile([P, 1], F32, name="sd_%d" % m)
+            nc.scalar.activation(out=t[("sd", m)][:], in_=t[("ss", m)][:], func=ACT.Sqrt, scale=1.0 / D, bias=eps_t[:])
+
+        def op_rs(m):
+            t[("rs", m)] = keep.tile([P, 1], F32, name="rs_%d" % m)
+            nc.vector.reciprocal(out=t[("rs", m)][:], in_=t[("sd", m)][:])
+
+        def op_stt(m):
+            t[("h", m)] = keep.tile([P, D], BF16, name="h_%d" % m)
+            nc.vector.scalar_tensor_tensor(
+                out=t[("h", m)][:],
+                in0=x_sb[:, m, :],
+                scalar=t[("rs", m)][:, 0:1],
+                in1=t["wb"][:],
+                op0=ALU.mult,
+                op1=ALU.mult,
+            )
+
+        def op_tp(m):
+            tp = psum.tile([P, 4 * G, P], BF16, name="tp", tag="bank")
+            t[("tp", m)] = tp
+            for c in range(4 * G):
+                nc.tensor.transpose(tp[:, c, :], t[("h", m)][:, c * P : (c + 1) * P], ident[:])
+
+        def op_co(m):
+            if ("hg", m // 2) not in t:
+                t[("hg", m // 2)] = keep.tile([P, 2, G, P, 4], BF16, name="hg_%d" % (m // 2), align_bytes=64)
+            nc.scalar.copy(out=t[("hg", m // 2)][:, m % 2], in_=t[("tp", m)][:].rearrange("p (g t) r -> p g r t", g=G))
+
+        def op_qh(m0, m1):
+            nc.vector.quantize_mx(
+                out=h_codes[:, m0:m1, :].rearrange("p m c -> p (m c)").bitcast(FP8X4),
+                scales=h_scales[:, m0:m1, :].rearrange("p m c -> p (m c)"),
+                in_=t[("hg", m0 // 2)][:, m0 % 2 : m0 % 2 + m1 - m0].rearrange("p m g r t -> p (m g r t)"),
+            )
+
+        def op_mm(m, nb):
+            acc = psum.tile([P, NBW], F32, name="acc", tag="bank")
+            t[("acc", m, nb)] = acc
+            for g in range(G):
+                nc.tensor.matmul_mx(
+                    out=acc[:],
+                    lhsT=h_codes[:, m, g * P : (g + 1) * P].bitcast(FP8X4),
+                    lhsT_scale=h_scales[:, m, g * P : (g + 1) * P],
+                    rhs=w_codes[:, nb, g * NBW : (g + 1) * NBW].bitcast(FP8X4),
+                    rhs_scale=w_scales[:, nb, g * NBW : (g + 1) * NBW],
+                    start=(g == 0),
+                    stop=(g == G - 1),
+                )
+
+        def small(kind, j, nb):
+            key = (kind, j, nb)
+            if key not in t:
+                t[key] = keep.tile([P, 4], F32, name="%s_%d_%d" % (kind, j, nb))
+            return t[key]
+
+        def stage(j, nb):
+            key = ("st", j, nb)
+            if key not in t:
+                t[key] = keep.tile([P, 2, 2, HD], F32, name="st_%d_%d" % (j, nb))
+            return t[key]
+
+        def op_s2(m, nb, hh):
+            col = 2 * (m % 2) + hh
+            nc.scalar.activation(
+                out=junk[:, 0:HD],
+                in_=t[("acc", m, nb)][:, hh * HD : (hh + 1) * HD],
+                func=ACT.Square,
+                accum_out=small("ss4", m // 2, nb)[:, col : col + 1],
+            )
+
+        def op_sr(j, nb):
+            nc.scalar.activation(out=small("nr", j, nb)[:], in_=small("ss4", j, nb)[:], func=ACT.Sqrt)
+
+        def op_rc(j, nb):
+            nc.vector.reciprocal(out=small("rn", j, nb)[:], in_=small("nr", j, nb)[:])
+
+        def op_sc(m, nb):
+            i = m % 2
+            nc.vector.scalar_tensor_tensor(
+                out=stage(m // 2, nb)[:, :, i, :],
+                in0=small("rn", m // 2, nb)[:, 2 * i : 2 * i + 2].unsqueeze(2).to_broadcast([P, 2, HD]),
+                scalar=1.0 / EPS_NORM,
+                in1=t[("acc", m, nb)][:].rearrange("p (h d) -> p h d", h=2),
+                op0=ALU.min,
+                op1=ALU.mult,
+            )
+
+        def op_vcv(m):
+            nc.vector.tensor_copy(
+                out=stage(m // 2, 3)[:, :, m % 2, :], in_=t[("acc", m, 3)][:].rearrange("p (h d) -> p h d", h=2)
+            )
+
+        def op_vc(m):
+            nc.scalar.copy(
+                out=stage(m // 2, 3)[:, :, m % 2, :], in_=t[("acc", m, 3)][:].rearrange("p (h d) -> p h d", h=2)
+            )
+
+        def op_st(j, nb, i0, i1):
+            nc.sync.dma_start(out=out_views[nb][:, :, 2 * j + i0 : 2 * j + i1, :], in_=stage(j, nb)[:, :, i0:i1, :])
+
+        ops = {
+            "memset": op_memset, "ld_nw": op_ld_nw, "ld_x": op_ld_x, "ld_w": op_ld_w, "nwcopy": op_nwcopy,
+            "nwmm": op_nwmm, "R": op_R, "QW": op_QW, "sq": op_sq, "sd": op_sd, "rs": op_rs, "stt": op_stt,
+            "tp": op_tp, "co": op_co, "qh": op_qh, "mm": op_mm, "s2": op_s2, "sr": op_sr, "vcv": op_vcv,
+            "rc": op_rc, "sc": op_sc, "vc": op_vc, "st": op_st,
+        }
+        for op in ORDER:
+            ops[op[0]](*op[1:])

@@ -25,46 +25,48 @@ EPS_RMS = 1e-6
 EPS_NORM = 1e-12
 
 ORDER = [
-    ("memset",), ("ld_nw",), ("ld_w", 0, 0), ("ld_x", 0, 1), ("ld_x", 1, 2), ("ld_w", 0, 1),
-    ("ld_x", 2, 4), ("ld_w", 3, 0), ("ld_w", 3, 1), ("ld_x", 4, 6), ("ld_x", 6, 8), ("ld_w", 1, 0),
-    ("ld_w", 1, 1), ("ld_w", 2, 0), ("ld_w", 2, 1), ("nwcopy",), ("nwmm",), ("R", 0, 0),
-    ("sq", 0), ("sd", 0), ("sq", 1), ("rs", 0), ("stt", 0), ("sd", 1),
-    ("R", 0, 1), ("tp", 0), ("sq", 2), ("QW", 0), ("co", 0), ("rs", 1),
-    ("stt", 1), ("sd", 2), ("sq", 3), ("qh", 0, 1), ("tp", 1), ("sd", 3),
-    ("rs", 2), ("sq", 4), ("rs", 3), ("stt", 2), ("mm", 0, 0), ("co", 1),
-    ("stt", 3), ("tp", 2), ("s2", 0, 0, 0), ("qh", 1, 2), ("s2", 0, 0, 1), ("tp", 3),
-    ("R", 3, 0), ("co", 2), ("mm", 1, 0), ("R", 3, 1), ("co", 3), ("s2", 1, 0, 0),
-    ("QW", 3), ("s2", 1, 0, 1), ("sr", 0, 0), ("sd", 4), ("sq", 5), ("rc", 0, 0),
-    ("mm", 0, 3), ("sc", 0, 0), ("mm", 1, 3), ("sc", 1, 0), ("sd", 5), ("sq", 6),
-    ("qh", 2, 4), ("st", 0, 0, 0, 2), ("rs", 4), ("mm", 2, 0), ("sd", 6), ("rs", 5),
-    ("sq", 7), ("stt", 4), ("mm", 3, 0), ("mm", 2, 3), ("s2", 2, 0, 0), ("stt", 5),
-    ("s2", 2, 0, 1), ("tp", 4), ("s2", 3, 0, 0), ("s2", 3, 0, 1), ("rs", 6), ("stt", 6),
-    ("tp", 5), ("sr", 1, 0), ("co", 4), ("rc", 1, 0), ("co", 5), ("tp", 6),
-    ("sc", 2, 0), ("sc", 3, 0), ("mm", 3, 3), ("sd", 7), ("co", 6), ("qh", 4, 6),
-    ("st", 1, 0, 0, 2), ("rs", 7), ("mm", 4, 0), ("stt", 7), ("vc", 0), ("mm", 5, 0),
-    ("s2", 4, 0, 0), ("mm", 4, 3), ("R", 1, 0), ("s2", 4, 0, 1), ("s2", 5, 0, 0), ("tp", 7),
-    ("s2", 5, 0, 1), ("sr", 2, 0), ("R", 1, 1), ("vc", 1), ("mm", 5, 3), ("co", 7),
-    ("st", 0, 3, 0, 2), ("rc", 2, 0), ("sc", 4, 0), ("vc", 2), ("sc", 5, 0), ("vc", 3),
-    ("qh", 6, 8), ("st", 2, 0, 0, 2), ("vc", 4), ("st", 1, 3, 0, 2), ("QW", 1), ("mm", 6, 0),
-    ("vc", 5), ("mm", 7, 0), ("s2", 6, 0, 0), ("st", 2, 3, 0, 2), ("s2", 6, 0, 1), ("R", 2, 0),
-    ("mm", 6, 3), ("s2", 7, 0, 0), ("mm", 7, 3), ("s2", 7, 0, 1), ("sr", 3, 0), ("R", 2, 1),
-    ("mm", 0, 1), ("vc", 6), ("mm", 1, 1), ("vc", 7), ("mm", 2, 1), ("rc", 3, 0),
-    ("s2", 0, 1, 0), ("sc", 6, 0), ("st", 3, 3, 0, 2), ("s2", 0, 1, 1), ("mm", 3, 1), ("s2", 1, 1, 0),
-    ("sc", 7, 0), ("mm", 4, 1), ("s2", 1, 1, 1), ("QW", 2), ("sr", 0, 1), ("st", 3, 0, 0, 2),
-    ("s2", 2, 1, 0), ("mm", 5, 1), ("s2", 2, 1, 1), ("mm", 6, 1), ("s2", 3, 1, 0), ("rc", 0, 1),
-    ("s2", 3, 1, 1), ("sc", 0, 1), ("mm", 7, 1), ("sr", 1, 1), ("s2", 4, 1, 0), ("sc", 1, 1),
-    ("mm", 0, 2), ("s2", 4, 1, 1), ("s2", 5, 1, 0), ("rc", 1, 1), ("mm", 1, 2), ("st", 0, 1, 0, 2),
-    ("sc", 2, 1), ("s2", 5, 1, 1), ("sr", 2, 1), ("s2", 6, 1, 0), ("sc", 3, 1), ("mm", 2, 2),
-    ("s2", 6, 1, 1), ("rc", 2, 1), ("mm", 3, 2), ("s2", 7, 1, 0), ("st", 1, 1, 0, 2), ("sc", 4, 1),
-    ("s2", 7, 1, 1), ("sc", 5, 1), ("mm", 4, 2), ("sr", 3, 1), ("s2", 0, 2, 0), ("s2", 0, 2, 1),
-    ("rc", 3, 1), ("mm", 5, 2), ("st", 2, 1, 0, 2), ("sc", 6, 1), ("s2", 1, 2, 0), ("s2", 1, 2, 1),
-    ("sc", 7, 1), ("mm", 6, 2), ("sr", 0, 2), ("s2", 2, 2, 0), ("rc", 0, 2), ("mm", 7, 2),
-    ("s2", 2, 2, 1), ("st", 3, 1, 0, 2), ("sc", 0, 2), ("s2", 3, 2, 0), ("sc", 1, 2), ("s2", 3, 2, 1),
-    ("sr", 1, 2), ("s2", 4, 2, 0), ("rc", 1, 2), ("st", 0, 2, 0, 2), ("sc", 2, 2), ("s2", 4, 2, 1),
-    ("s2", 5, 2, 0), ("sc", 3, 2), ("s2", 5, 2, 1), ("sr", 2, 2), ("s2", 6, 2, 0), ("st", 1, 2, 0, 2),
-    ("rc", 2, 2), ("sc", 4, 2), ("s2", 6, 2, 1), ("s2", 7, 2, 0), ("sc", 5, 2), ("s2", 7, 2, 1),
-    ("sr", 3, 2), ("st", 2, 2, 0, 2), ("rc", 3, 2), ("sc", 6, 2), ("sc", 7, 2), ("st", 3, 2, 0, 1),
-    ("st", 3, 2, 1, 2),
+    ("memset",), ("ld_nw",), ("ld_x", 0, 1), ("ld_w", 3, 0), ("ld_x", 1, 2), ("ld_w", 3, 1),
+    ("ld_x", 2, 4), ("ld_x", 4, 6), ("ld_x", 6, 8), ("ld_w", 0, 0), ("ld_w", 0, 1), ("ld_w", 1, 0),
+    ("ld_w", 1, 1), ("ld_w", 2, 0), ("ld_w", 2, 1), ("nwcopy",), ("nwmm",), ("sq", 0),
+    ("wbc",), ("sd", 0), ("R", 3, 0), ("sq", 1), ("rs", 0), ("stt", 0),
+    ("sd", 1), ("R", 3, 1), ("tp", 0), ("QW", 3), ("sq", 2), ("rs", 1),
+    ("stt", 1), ("co", 0), ("sd", 2), ("tp", 1), ("sq", 3), ("qh", 0, 1),
+    ("rs", 2), ("stt", 2), ("mm", 0, 3), ("sd", 3), ("sq", 4), ("rs", 3),
+    ("stt", 3), ("tp", 2), ("co", 1), ("R", 0, 0), ("tp", 3), ("vc", 0),
+    ("qh", 1, 2), ("co", 2), ("R", 0, 1), ("mm", 1, 3), ("co", 3), ("QW", 0),
+    ("vc", 1), ("qh", 2, 4), ("sd", 4), ("mm", 0, 0), ("sq", 5), ("st", 0, 3, 0, 2),
+    ("R", 1, 0), ("mm", 2, 3), ("sd", 5), ("sq", 6), ("rs", 4), ("stt", 4),
+    ("mm", 3, 3), ("vc", 2), ("mm", 1, 0), ("rs", 5), ("stt", 5), ("vc", 3),
+    ("tp", 4), ("sd", 6), ("sq", 7), ("R", 1, 1), ("st", 1, 3, 0, 2), ("tp", 5),
+    ("sd", 7), ("rs", 6), ("co", 4), ("stt", 6), ("mm", 2, 0), ("co", 5),
+    ("rs", 7), ("stt", 7), ("tp", 6), ("s2", 0, 0, 0), ("QW", 1), ("s2", 0, 0, 1),
+    ("tp", 7), ("s2", 1, 0, 0), ("co", 6), ("qh", 4, 6), ("mm", 3, 0), ("R", 2, 0),
+    ("co", 7), ("mm", 4, 3), ("R", 2, 1), ("s2", 1, 0, 1), ("mm", 5, 3), ("sr", 0, 0),
+    ("s2", 2, 0, 0), ("vc", 4), ("qh", 6, 8), ("mm", 4, 0), ("s2", 2, 0, 1), ("QW", 2),
+    ("vc", 5), ("mm", 6, 3), ("s2", 3, 0, 0), ("st", 2, 3, 0, 2), ("s2", 3, 0, 1), ("mx", 0, 0),
+    ("rc", 0, 0), ("sc", 0, 0), ("sr", 1, 0), ("mm", 7, 3), ("s2", 4, 0, 0), ("vc", 6),
+    ("sc", 1, 0), ("mm", 5, 0), ("s2", 4, 0, 1), ("mx", 1, 0), ("rc", 1, 0), ("sc", 2, 0),
+    ("vc", 7), ("st", 0, 0, 0, 2), ("mm", 6, 0), ("sc", 3, 0), ("s2", 5, 0, 0), ("st", 3, 3, 0, 2),
+    ("s2", 5, 0, 1), ("st", 1, 0, 0, 2), ("mm", 7, 0), ("sr", 2, 0), ("s2", 6, 0, 0), ("mx", 2, 0),
+    ("rc", 2, 0), ("sc", 4, 0), ("s2", 6, 0, 1), ("mm", 0, 1), ("sc", 5, 0), ("s2", 7, 0, 0),
+    ("s2", 7, 0, 1), ("mm", 1, 1), ("sr", 3, 0), ("st", 2, 0, 0, 2), ("s2", 0, 1, 0), ("mx", 3, 0),
+    ("rc", 3, 0), ("sc", 6, 0), ("s2", 0, 1, 1), ("mm", 2, 1), ("sc", 7, 0), ("s2", 1, 1, 0),
+    ("s2", 1, 1, 1), ("mm", 3, 1), ("sr", 0, 1), ("st", 3, 0, 0, 2), ("s2", 2, 1, 0), ("mx", 0, 1),
+    ("rc", 0, 1), ("sc", 0, 1), ("s2", 2, 1, 1), ("mm", 4, 1), ("sc", 1, 1), ("s2", 3, 1, 0),
+    ("s2", 3, 1, 1), ("mm", 5, 1), ("sr", 1, 1), ("st", 0, 1, 0, 2), ("s2", 4, 1, 0), ("mx", 1, 1),
+    ("rc", 1, 1), ("sc", 2, 1), ("s2", 4, 1, 1), ("mm", 6, 1), ("sc", 3, 1), ("s2", 5, 1, 0),
+    ("s2", 5, 1, 1), ("mm", 7, 1), ("sr", 2, 1), ("st", 1, 1, 0, 2), ("s2", 6, 1, 0), ("mx", 2, 1),
+    ("rc", 2, 1), ("sc", 4, 1), ("s2", 6, 1, 1), ("mm", 0, 2), ("sc", 5, 1), ("s2", 7, 1, 0),
+    ("s2", 7, 1, 1), ("mm", 1, 2), ("sr", 3, 1), ("st", 2, 1, 0, 2), ("s2", 0, 2, 0), ("mx", 3, 1),
+    ("rc", 3, 1), ("sc", 6, 1), ("s2", 0, 2, 1), ("mm", 2, 2), ("sc", 7, 1), ("s2", 1, 2, 0),
+    ("s2", 1, 2, 1), ("mm", 3, 2), ("sr", 0, 2), ("st", 3, 1, 0, 2), ("s2", 2, 2, 0), ("mx", 0, 2),
+    ("rc", 0, 2), ("sc", 0, 2), ("s2", 2, 2, 1), ("mm", 4, 2), ("sc", 1, 2), ("s2", 3, 2, 0),
+    ("s2", 3, 2, 1), ("mm", 5, 2), ("sr", 1, 2), ("st", 0, 2, 0, 2), ("s2", 4, 2, 0), ("mx", 1, 2),
+    ("rc", 1, 2), ("sc", 2, 2), ("s2", 4, 2, 1), ("mm", 6, 2), ("sc", 3, 2), ("s2", 5, 2, 0),
+    ("s2", 5, 2, 1), ("mm", 7, 2), ("sr", 2, 2), ("st", 1, 2, 0, 2), ("s2", 6, 2, 0), ("mx", 2, 2),
+    ("rc", 2, 2), ("sc", 4, 2), ("s2", 6, 2, 1), ("sc", 5, 2), ("s2", 7, 2, 0), ("s2", 7, 2, 1),
+    ("sr", 3, 2), ("st", 2, 2, 0, 2), ("mx", 3, 2), ("rc", 3, 2), ("sc", 6, 2), ("sc", 7, 2),
+    ("st", 3, 2, 0, 1), ("st", 3, 2, 1, 2),
 ]
 
 
@@ -130,6 +132,10 @@ def tile_sharedglobalattention_pa_kernel(tc, x, norm_w, Wq, Wk, Wv, out_0, out_1
                 cols = slice(half * 512, (half + 1) * 512)
                 nc.tensor.matmul(t["wb"][:, cols], lhsT=ones[:], rhs=nw_row[:, cols], start=True, stop=True)
 
+        def op_wbc():
+            t["wb_sb"] = keep.tile([P, D], BF16, name="wb_sb")
+            nc.vector.tensor_copy(out=t["wb_sb"][:], in_=t["wb"][:])
+
         def op_R(nb, g):
             if ("wg", nb) not in t:
                 t[("wg", nb)] = keep.tile([P, G, NBW, 4], BF16, name="wg_%d" % nb, align_bytes=64)
@@ -163,7 +169,7 @@ def tile_sharedglobalattention_pa_kernel(tc, x, norm_w, Wq, Wk, Wv, out_0, out_1
                 out=t[("h", m)][:],
                 in0=x_sb[:, m, :],
                 scalar=t[("rs", m)][:, 0:1],
-                in1=t["wb"][:],
+                in1=t["wb_sb"][:],
                 op0=ALU.mult,
                 op1=ALU.mult,
             )
@@ -224,18 +230,19 @@ def tile_sharedglobalattention_pa_kernel(tc, x, norm_w, Wq, Wk, Wv, out_0, out_1
         def op_sr(j, nb):
             nc.scalar.activation(out=small("nr", j, nb)[:], in_=small("ss4", j, nb)[:], func=ACT.Sqrt)
 
+        def op_mx(j, nb):
+            nc.vector.tensor_scalar_max(out=small("nm", j, nb)[:], in0=small("nr", j, nb)[:], scalar1=EPS_NORM)
+
         def op_rc(j, nb):
-            nc.vector.reciprocal(out=small("rn", j, nb)[:], in_=small("nr", j, nb)[:])
+            nc.vector.reciprocal(out=small("rn", j, nb)[:], in_=small("nm", j, nb)[:])
 
         def op_sc(m, nb):
             i = m % 2
-            nc.vector.scalar_tensor_tensor(
+            nc.vector.tensor_tensor(
                 out=stage(m // 2, nb)[:, :, i, :],
-                in0=small("rn", m // 2, nb)[:, 2 * i : 2 * i + 2].unsqueeze(2).to_broadcast([P, 2, HD]),
-                scalar=1.0 / EPS_NORM,
-                in1=t[("acc", m, nb)][:].rearrange("p (h d) -> p h d", h=2),
-                op0=ALU.min,
-                op1=ALU.mult,
+                in0=t[("acc", m, nb)][:].rearrange("p (h d) -> p h d", h=2),
+                in1=small("rn", m // 2, nb)[:, 2 * i : 2 * i + 2].unsqueeze(2).to_broadcast([P, 2, HD]),
+                op=ALU.mult,
             )
 
         def op_vcv(m):
@@ -254,7 +261,7 @@ def tile_sharedglobalattention_pa_kernel(tc, x, norm_w, Wq, Wk, Wv, out_0, out_1
         ops = {
             "memset": op_memset, "ld_nw": op_ld_nw, "ld_x": op_ld_x, "ld_w": op_ld_w, "nwcopy": op_nwcopy,
             "nwmm": op_nwmm, "R": op_R, "QW": op_QW, "sq": op_sq, "sd": op_sd, "rs": op_rs, "stt": op_stt,
-            "tp": op_tp, "co": op_co, "qh": op_qh, "mm": op_mm, "s2": op_s2, "sr": op_sr, "vcv": op_vcv,
+            "tp": op_tp, "co": op_co, "qh": op_qh, "mm": op_mm, "s2": op_s2, "sr": op_sr, "vcv": op_vcv, "mx": op_mx, "wbc": op_wbc,
             "rc": op_rc, "sc": op_sc, "vc": op_vc, "st": op_st,
         }
         for op in ORDER:

@@ -24,73 +24,31 @@ G = 2
 EPS_RMS = 1e-6
 EPS_NORM = 1e-12
 
-ORDER = [
-    ("memset",), ("ld_nw",), ("ld_x", 0, 1), ("ld_w", 3, 0), ("ld_x", 1, 2), ("ld_w", 3, 1),
-    ("ld_x", 2, 4), ("ld_x", 4, 6), ("ld_x", 6, 8), ("ld_w", 0, 0), ("ld_w", 0, 1), ("ld_w", 1, 0),
-    ("ld_w", 1, 1), ("ld_w", 2, 0), ("ld_w", 2, 1), ("nwcopy",), ("nwmm",), ("sq", 0),
-    ("wbc",), ("sd", 0), ("R", 3, 0), ("sq", 1), ("rs", 0), ("stt", 0),
-    ("sd", 1), ("R", 3, 1), ("tp", 0), ("QW", 3), ("sq", 2), ("rs", 1),
-    ("stt", 1), ("co", 0), ("sd", 2), ("tp", 1), ("sq", 3), ("qh", 0, 1),
-    ("rs", 2), ("stt", 2), ("mm", 0, 3), ("sd", 3), ("sq", 4), ("rs", 3),
-    ("stt", 3), ("tp", 2), ("co", 1), ("R", 0, 0), ("tp", 3), ("vc", 0),
-    ("qh", 1, 2), ("co", 2), ("R", 0, 1), ("mm", 1, 3), ("co", 3), ("QW", 0),
-    ("vc", 1), ("qh", 2, 4), ("sd", 4), ("mm", 0, 0), ("sq", 5), ("st", 0, 3, 0, 2),
-    ("R", 1, 0), ("mm", 2, 3), ("sd", 5), ("sq", 6), ("rs", 4), ("stt", 4),
-    ("mm", 3, 3), ("vc", 2), ("mm", 1, 0), ("rs", 5), ("stt", 5), ("vc", 3),
-    ("tp", 4), ("sd", 6), ("sq", 7), ("R", 1, 1), ("st", 1, 3, 0, 2), ("tp", 5),
-    ("sd", 7), ("rs", 6), ("co", 4), ("stt", 6), ("mm", 2, 0), ("co", 5),
-    ("rs", 7), ("stt", 7), ("tp", 6), ("s2", 0, 0, 0), ("QW", 1), ("s2", 0, 0, 1),
-    ("tp", 7), ("s2", 1, 0, 0), ("co", 6), ("qh", 4, 6), ("mm", 3, 0), ("R", 2, 0),
-    ("co", 7), ("mm", 4, 3), ("R", 2, 1), ("s2", 1, 0, 1), ("mm", 5, 3), ("sr", 0, 0),
-    ("s2", 2, 0, 0), ("vc", 4), ("qh", 6, 8), ("mm", 4, 0), ("s2", 2, 0, 1), ("QW", 2),
-    ("vc", 5), ("mm", 6, 3), ("s2", 3, 0, 0), ("st", 2, 3, 0, 2), ("s2", 3, 0, 1), ("mx", 0, 0),
-    ("rc", 0, 0), ("sc", 0, 0), ("sr", 1, 0), ("mm", 7, 3), ("s2", 4, 0, 0), ("vc", 6),
-    ("sc", 1, 0), ("mm", 5, 0), ("s2", 4, 0, 1), ("mx", 1, 0), ("rc", 1, 0), ("sc", 2, 0),
-    ("vc", 7), ("st", 0, 0, 0, 2), ("mm", 6, 0), ("sc", 3, 0), ("s2", 5, 0, 0), ("st", 3, 3, 0, 2),
-    ("s2", 5, 0, 1), ("st", 1, 0, 0, 2), ("mm", 7, 0), ("sr", 2, 0), ("s2", 6, 0, 0), ("mx", 2, 0),
-    ("rc", 2, 0), ("sc", 4, 0), ("s2", 6, 0, 1), ("mm", 0, 1), ("sc", 5, 0), ("s2", 7, 0, 0),
-    ("s2", 7, 0, 1), ("mm", 1, 1), ("sr", 3, 0), ("st", 2, 0, 0, 2), ("s2", 0, 1, 0), ("mx", 3, 0),
-    ("rc", 3, 0), ("sc", 6, 0), ("s2", 0, 1, 1), ("mm", 2, 1), ("sc", 7, 0), ("s2", 1, 1, 0),
-    ("s2", 1, 1, 1), ("mm", 3, 1), ("sr", 0, 1), ("st", 3, 0, 0, 2), ("s2", 2, 1, 0), ("mx", 0, 1),
-    ("rc", 0, 1), ("sc", 0, 1), ("s2", 2, 1, 1), ("mm", 4, 1), ("sc", 1, 1), ("s2", 3, 1, 0),
-    ("s2", 3, 1, 1), ("mm", 5, 1), ("sr", 1, 1), ("st", 0, 1, 0, 2), ("s2", 4, 1, 0), ("mx", 1, 1),
-    ("rc", 1, 1), ("sc", 2, 1), ("s2", 4, 1, 1), ("mm", 6, 1), ("sc", 3, 1), ("s2", 5, 1, 0),
-    ("s2", 5, 1, 1), ("mm", 7, 1), ("sr", 2, 1), ("st", 1, 1, 0, 2), ("s2", 6, 1, 0), ("mx", 2, 1),
-    ("rc", 2, 1), ("sc", 4, 1), ("s2", 6, 1, 1), ("mm", 0, 2), ("sc", 5, 1), ("s2", 7, 1, 0),
-    ("s2", 7, 1, 1), ("mm", 1, 2), ("sr", 3, 1), ("st", 2, 1, 0, 2), ("s2", 0, 2, 0), ("mx", 3, 1),
-    ("rc", 3, 1), ("sc", 6, 1), ("s2", 0, 2, 1), ("mm", 2, 2), ("sc", 7, 1), ("s2", 1, 2, 0),
-    ("s2", 1, 2, 1), ("mm", 3, 2), ("sr", 0, 2), ("st", 3, 1, 0, 2), ("s2", 2, 2, 0), ("mx", 0, 2),
-    ("rc", 0, 2), ("sc", 0, 2), ("s2", 2, 2, 1), ("mm", 4, 2), ("sc", 1, 2), ("s2", 3, 2, 0),
-    ("s2", 3, 2, 1), ("mm", 5, 2), ("sr", 1, 2), ("st", 0, 2, 0, 2), ("s2", 4, 2, 0), ("mx", 1, 2),
-    ("rc", 1, 2), ("sc", 2, 2), ("s2", 4, 2, 1), ("mm", 6, 2), ("sc", 3, 2), ("s2", 5, 2, 0),
-    ("s2", 5, 2, 1), ("mm", 7, 2), ("sr", 2, 2), ("st", 1, 2, 0, 2), ("s2", 6, 2, 0), ("mx", 2, 2),
-    ("rc", 2, 2), ("sc", 4, 2), ("s2", 6, 2, 1), ("sc", 5, 2), ("s2", 7, 2, 0), ("s2", 7, 2, 1),
-    ("sr", 3, 2), ("st", 2, 2, 0, 2), ("mx", 3, 2), ("rc", 3, 2), ("sc", 6, 2), ("sc", 7, 2),
-    ("st", 3, 2, 0, 1), ("st", 3, 2, 1, 2),
-]
-
 
 def tile_sharedglobalattention_pa_kernel(tc, x, norm_w, Wq, Wk, Wv, out_0, out_1, out_2):
     nc = tc.nc
     with ExitStack() as ctx:
         keep = ctx.enter_context(tc.tile_pool(name="keep", bufs=1))
-        psum = ctx.enter_context(tc.psum_pool(name="psum", bufs=8))
-        ctx.enter_context(tc.manual_schedule())
+        stage_pool = ctx.enter_context(tc.tile_pool(name="stage", bufs=1))
+        work = ctx.enter_context(tc.tile_pool(name="work", bufs=3))
+        small = ctx.enter_context(tc.tile_pool(name="small", bufs=4))
+        psum = ctx.enter_context(tc.psum_pool(name="psum", bufs=7))
+        psum_w = ctx.enter_context(tc.psum_pool(name="psum_w", bufs=1))
 
         eps_t = keep.tile([P, 1], F32, name="eps_t")
+        nc.vector.memset(eps_t[:], EPS_RMS)
         warm = keep.tile([P, 1], F32, name="warm")
-        nw_in = keep.tile([1, D], BF16, name="nw_in")
+        nc.scalar.activation(out=warm[:], in_=eps_t[:], func=ACT.Sqrt)
         nw_row = keep.tile([P, D], BF16, name="nw_row")
+        nc.vector.memset(nw_row[:], 0.0)
         ones = keep.tile([P, P], BF16, name="ones")
+        nc.vector.memset(ones[:], 1.0)
         ident = keep.tile([P, P], BF16, name="ident")
-        x_sb = keep.tile([P, MT, D], BF16, name="x_sb")
-        w_raw = [keep.tile([P, 4 * G, NBW], BF16, name="w_raw%d" % nb) for nb in range(NB)]
-        h_codes = keep.tile([P, MT, G * P], U32, name="h_codes", align_bytes=64)
-        h_scales = keep.tile([P, MT, G * P], U8, name="h_scales", align_bytes=64)
-        w_codes = keep.tile([P, NB, G * NBW], U32, name="w_codes", align_bytes=64)
-        w_scales = keep.tile([P, NB, G * NBW], U8, name="w_scales", align_bytes=64)
-        junk = keep.tile([P, D], BF16, name="junk")
+        make_identity(nc, ident[:])
 
+        nw_in = keep.tile([1, D], BF16, name="nw_in")
+        nc.sync.dma_start(out=nw_in[:], in_=norm_w.rearrange("(o k) -> o k", o=1))
+        x_sb = keep.tile([P, MT, D], BF16, name="x_sb")
         x_view = x.rearrange("b (p m) k -> p (b m) k", m=MT)
         w_src = [
             Wq[:, 0:NBW].rearrange("(c p) n -> p c n", p=P),
@@ -98,171 +56,142 @@ def tile_sharedglobalattention_pa_kernel(tc, x, norm_w, Wq, Wk, Wv, out_0, out_1
             Wk.rearrange("(c p) n -> p c n", p=P),
             Wv.rearrange("(c p) n -> p c n", p=P),
         ]
+        w_raw = [keep.tile([P, 4 * G, NBW], BF16, name="w_raw%d" % nb) for nb in range(NB)]
+
+        def load_x(m0, m1):
+            nc.sync.dma_start(out=x_sb[:, m0:m1, :], in_=x_view[:, m0:m1, :])
+
+        def load_w(nb, g):
+            rows = slice(4 * g, 4 * g + 4)
+            nc.sync.dma_start(out=w_raw[nb][:, rows, :], in_=w_src[nb][:, rows, :])
+
+        load_w(0, 0)
+        load_x(0, 1)
+        load_x(1, 2)
+        load_w(0, 1)
+        load_x(2, 4)
+        load_w(3, 0)
+        load_w(3, 1)
+        load_x(4, 6)
+        load_x(6, 8)
+        load_w(1, 0)
+        load_w(1, 1)
+        load_w(2, 0)
+        load_w(2, 1)
+
+        nc.vector.tensor_copy(out=nw_row[0:1, :], in_=nw_in[:])
+        wb = psum_w.tile([P, D], BF16, name="wb")
+        for half in range(2):
+            cols = slice(half * 512, (half + 1) * 512)
+            nc.tensor.matmul(wb[:, cols], lhsT=ones[:], rhs=nw_row[:, cols], start=True, stop=True)
+
+        h_codes = keep.tile([P, MT, G * P], U32, name="h_codes", align_bytes=64)
+        h_scales = keep.tile([P, MT, G * P], U8, name="h_scales", align_bytes=64)
+        w_codes = keep.tile([P, NB, G, NBW], U32, name="w_codes", align_bytes=64)
+        w_scales = keep.tile([P, NB, G, NBW], U8, name="w_scales", align_bytes=64)
+
+        def prep_w(nb):
+            grouped = []
+            for g in range(G):
+                wg = work.tile([P, NBW, 4], BF16, name="wg", tag="wg", bufs=4, align_bytes=64)
+                nc.vector.tensor_copy(
+                    out=wg[:].rearrange("p (c i) t -> p c t i", i=4),
+                    in_=w_raw[nb][:, 4 * g : 4 * g + 4, :].rearrange("p t (c i) -> p c t i", i=4),
+                )
+                grouped.append(wg)
+            for g in range(G):
+                nc.vector.quantize_mx(
+                    out=w_codes[:, nb, g, :].bitcast(FP8X4),
+                    scales=w_scales[:, nb, g, :],
+                    in_=grouped[g][:].rearrange("p n t -> p (n t)"),
+                )
+
+        def stats(m):
+            junk = work.tile([P, D], BF16, name="junk", tag="junk", bufs=4)
+            ss = small.tile([P, 1], F32, name="ss", tag="ss")
+            nc.scalar.activation(out=junk[:], in_=x_sb[:, m, :], func=ACT.Square, accum_out=ss[:])
+            sd = small.tile([P, 1], F32, name="sd", tag="sd")
+            nc.scalar.activation(out=sd[:], in_=ss[:], func=ACT.Sqrt, scale=1.0 / D, bias=eps_t[:])
+            rstd = small.tile([P, 1], F32, name="rstd", tag="rstd")
+            nc.vector.reciprocal(out=rstd[:], in_=sd[:])
+            return rstd
+
+        def prep_h(m, rstd):
+            h_sb = work.tile([P, D], BF16, name="h_sb", tag="h_sb")
+            nc.vector.scalar_tensor_tensor(
+                out=h_sb[:], in0=x_sb[:, m, :], scalar=rstd[:, 0:1], in1=wb[:], op0=ALU.mult, op1=ALU.mult
+            )
+            tp = psum.tile([P, 4 * G, P], BF16, name="tp", tag="bank")
+            for c in range(4 * G):
+                nc.tensor.transpose(tp[:, c, :], h_sb[:, c * P : (c + 1) * P], ident[:])
+            hg = work.tile([P, G, P, 4], BF16, name="hg", tag="hg", align_bytes=64)
+            nc.scalar.copy(out=hg[:], in_=tp[:].rearrange("p (g t) r -> p g r t", g=G))
+            nc.vector.quantize_mx(
+                out=h_codes[:, m, :].bitcast(FP8X4),
+                scales=h_scales[:, m, :],
+                in_=hg[:].rearrange("p g r t -> p (g r t)"),
+            )
+
+        def project(m, nb):
+            acc = psum.tile([P, NBW], F32, name="acc", tag="bank")
+            for g in range(G):
+                nc.tensor.matmul_mx(
+                    out=acc[:],
+                    lhsT=h_codes[:, m, g * P : (g + 1) * P].bitcast(FP8X4),
+                    lhsT_scale=h_scales[:, m, g * P : (g + 1) * P],
+                    rhs=w_codes[:, nb, g, :].bitcast(FP8X4),
+                    rhs_scale=w_scales[:, nb, g, :],
+                    start=(g == 0),
+                    stop=(g == G - 1),
+                )
+            return acc
+
         out_views = [
             out_0.rearrange("b h (p m) d -> p (b h) m d", m=MT)[:, 0:2],
             out_0.rearrange("b h (p m) d -> p (b h) m d", m=MT)[:, 2:4],
             out_1.rearrange("b h (p m) d -> p (b h) m d", m=MT),
             out_2.rearrange("b h (p m) d -> p (b h) m d", m=MT),
         ]
-        t = {}
 
-        def op_memset():
-            nc.vector.memset(eps_t[:], EPS_RMS)
-            nc.scalar.activation(out=warm[:], in_=eps_t[:], func=ACT.Sqrt)
-            nc.vector.memset(nw_row[:], 0.0)
-            nc.vector.memset(ones[:], 1.0)
-            make_identity(nc, ident[:])
+        def out_pair(j, nb):
+            st = stage_pool.tile([P, 2, 2, HD], F32, name="st_%d_%d" % (nb, j))
+            accs = [project(2 * j + i, nb) for i in range(2)]
+            if nb < 3:
+                ss4 = small.tile([P, 4], F32, name="ss4", tag="ss4")
+                for i in range(2):
+                    for hh in range(2):
+                        jq = work.tile([P, HD], BF16, name="jq", tag="jq", bufs=4)
+                        nc.scalar.activation(
+                            out=jq[:],
+                            in_=accs[i][:, hh * HD : (hh + 1) * HD],
+                            func=ACT.Square,
+                            accum_out=ss4[:, 2 * i + hh : 2 * i + hh + 1],
+                        )
+                nr = small.tile([P, 4], F32, name="nr", tag="nr")
+                nc.scalar.activation(out=nr[:], in_=ss4[:], func=ACT.Sqrt)
+                rn = small.tile([P, 4], F32, name="rn", tag="rn")
+                nc.vector.reciprocal(out=rn[:], in_=nr[:])
+                for i in range(2):
+                    nc.vector.scalar_tensor_tensor(
+                        out=st[:, :, i, :],
+                        in0=rn[:, 2 * i : 2 * i + 2].unsqueeze(2).to_broadcast([P, 2, HD]),
+                        scalar=1.0 / EPS_NORM,
+                        in1=accs[i][:].rearrange("p (h d) -> p h d", h=2),
+                        op0=ALU.min,
+                        op1=ALU.mult,
+                    )
+            else:
+                nc.scalar.copy(out=st[:, :, 0, :], in_=accs[0][:].rearrange("p (h d) -> p h d", h=2))
+                nc.scalar.copy(out=st[:, :, 1, :], in_=accs[1][:].rearrange("p (h d) -> p h d", h=2))
+            nc.sync.dma_start(out=out_views[nb][:, :, 2 * j : 2 * j + 2, :], in_=st[:])
 
-        def op_ld_nw():
-            nc.sync.dma_start(out=nw_in[:], in_=norm_w.rearrange("(o k) -> o k", o=1))
-
-        def op_ld_x(m0, m1):
-            nc.sync.dma_start(out=x_sb[:, m0:m1, :], in_=x_view[:, m0:m1, :])
-
-        def op_ld_w(nb, g):
-            rows = slice(4 * g, 4 * g + 4)
-            nc.sync.dma_start(out=w_raw[nb][:, rows, :], in_=w_src[nb][:, rows, :])
-
-        def op_nwcopy():
-            nc.vector.tensor_copy(out=nw_row[0:1, :], in_=nw_in[:])
-
-        def op_nwmm():
-            t["wb"] = psum.tile([P, D], BF16, name="wb", tag="bank")
-            for half in range(2):
-                cols = slice(half * 512, (half + 1) * 512)
-                nc.tensor.matmul(t["wb"][:, cols], lhsT=ones[:], rhs=nw_row[:, cols], start=True, stop=True)
-
-        def op_wbc():
-            t["wb_sb"] = keep.tile([P, D], BF16, name="wb_sb")
-            nc.vector.tensor_copy(out=t["wb_sb"][:], in_=t["wb"][:])
-
-        def op_R(nb, g):
-            if ("wg", nb) not in t:
-                t[("wg", nb)] = keep.tile([P, G, NBW, 4], BF16, name="wg_%d" % nb, align_bytes=64)
-            nc.vector.tensor_copy(
-                out=t[("wg", nb)][:, g].rearrange("p (c i) t -> p c t i", i=4),
-                in_=w_raw[nb][:, 4 * g : 4 * g + 4, :].rearrange("p t (c i) -> p c t i", i=4),
-            )
-
-        def op_QW(nb):
-            nc.vector.quantize_mx(
-                out=w_codes[:, nb, :].bitcast(FP8X4),
-                scales=w_scales[:, nb, :],
-                in_=t[("wg", nb)][:].rearrange("p g n t -> p (g n t)"),
-            )
-
-        def op_sq(m):
-            t[("ss", m)] = keep.tile([P, 1], F32, name="ss_%d" % m)
-            nc.scalar.activation(out=junk[:], in_=x_sb[:, m, :], func=ACT.Square, accum_out=t[("ss", m)][:])
-
-        def op_sd(m):
-            t[("sd", m)] = keep.tile([P, 1], F32, name="sd_%d" % m)
-            nc.scalar.activation(out=t[("sd", m)][:], in_=t[("ss", m)][:], func=ACT.Sqrt, scale=1.0 / D, bias=eps_t[:])
-
-        def op_rs(m):
-            t[("rs", m)] = keep.tile([P, 1], F32, name="rs_%d" % m)
-            nc.vector.reciprocal(out=t[("rs", m)][:], in_=t[("sd", m)][:])
-
-        def op_stt(m):
-            t[("h", m)] = keep.tile([P, D], BF16, name="h_%d" % m)
-            nc.vector.scalar_tensor_tensor(
-                out=t[("h", m)][:],
-                in0=x_sb[:, m, :],
-                scalar=t[("rs", m)][:, 0:1],
-                in1=t["wb_sb"][:],
-                op0=ALU.mult,
-                op1=ALU.mult,
-            )
-
-        def op_tp(m):
-            tp = psum.tile([P, 4 * G, P], BF16, name="tp", tag="bank")
-            t[("tp", m)] = tp
-            for c in range(4 * G):
-                nc.tensor.transpose(tp[:, c, :], t[("h", m)][:, c * P : (c + 1) * P], ident[:])
-
-        def op_co(m):
-            if ("hg", m // 2) not in t:
-                t[("hg", m // 2)] = keep.tile([P, 2, G, P, 4], BF16, name="hg_%d" % (m // 2), align_bytes=64)
-            nc.scalar.copy(out=t[("hg", m // 2)][:, m % 2], in_=t[("tp", m)][:].rearrange("p (g t) r -> p g r t", g=G))
-
-        def op_qh(m0, m1):
-            nc.vector.quantize_mx(
-                out=h_codes[:, m0:m1, :].rearrange("p m c -> p (m c)").bitcast(FP8X4),
-                scales=h_scales[:, m0:m1, :].rearrange("p m c -> p (m c)"),
-                in_=t[("hg", m0 // 2)][:, m0 % 2 : m0 % 2 + m1 - m0].rearrange("p m g r t -> p (m g r t)"),
-            )
-
-        def op_mm(m, nb):
-            acc = psum.tile([P, NBW], F32, name="acc", tag="bank")
-            t[("acc", m, nb)] = acc
-            for g in range(G):
-                nc.tensor.matmul_mx(
-                    out=acc[:],
-                    lhsT=h_codes[:, m, g * P : (g + 1) * P].bitcast(FP8X4),
-                    lhsT_scale=h_scales[:, m, g * P : (g + 1) * P],
-                    rhs=w_codes[:, nb, g * NBW : (g + 1) * NBW].bitcast(FP8X4),
-                    rhs_scale=w_scales[:, nb, g * NBW : (g + 1) * NBW],
-                    start=(g == 0),
-                    stop=(g == G - 1),
-                )
-
-        def small(kind, j, nb):
-            key = (kind, j, nb)
-            if key not in t:
-                t[key] = keep.tile([P, 4], F32, name="%s_%d_%d" % (kind, j, nb))
-            return t[key]
-
-        def stage(j, nb):
-            key = ("st", j, nb)
-            if key not in t:
-                t[key] = keep.tile([P, 2, 2, HD], F32, name="st_%d_%d" % (j, nb))
-            return t[key]
-
-        def op_s2(m, nb, hh):
-            col = 2 * (m % 2) + hh
-            nc.scalar.activation(
-                out=junk[:, 0:HD],
-                in_=t[("acc", m, nb)][:, hh * HD : (hh + 1) * HD],
-                func=ACT.Square,
-                accum_out=small("ss4", m // 2, nb)[:, col : col + 1],
-            )
-
-        def op_sr(j, nb):
-            nc.scalar.activation(out=small("nr", j, nb)[:], in_=small("ss4", j, nb)[:], func=ACT.Sqrt)
-
-        def op_mx(j, nb):
-            nc.vector.tensor_scalar_max(out=small("nm", j, nb)[:], in0=small("nr", j, nb)[:], scalar1=EPS_NORM)
-
-        def op_rc(j, nb):
-            nc.vector.reciprocal(out=small("rn", j, nb)[:], in_=small("nm", j, nb)[:])
-
-        def op_sc(m, nb):
-            i = m % 2
-            nc.vector.tensor_tensor(
-                out=stage(m // 2, nb)[:, :, i, :],
-                in0=t[("acc", m, nb)][:].rearrange("p (h d) -> p h d", h=2),
-                in1=small("rn", m // 2, nb)[:, 2 * i : 2 * i + 2].unsqueeze(2).to_broadcast([P, 2, HD]),
-                op=ALU.mult,
-            )
-
-        def op_vcv(m):
-            nc.vector.tensor_copy(
-                out=stage(m // 2, 3)[:, :, m % 2, :], in_=t[("acc", m, 3)][:].rearrange("p (h d) -> p h d", h=2)
-            )
-
-        def op_vc(m):
-            nc.scalar.copy(
-                out=stage(m // 2, 3)[:, :, m % 2, :], in_=t[("acc", m, 3)][:].rearrange("p (h d) -> p h d", h=2)
-            )
-
-        def op_st(j, nb, i0, i1):
-            nc.sync.dma_start(out=out_views[nb][:, :, 2 * j + i0 : 2 * j + i1, :], in_=stage(j, nb)[:, :, i0:i1, :])
-
-        ops = {
-            "memset": op_memset, "ld_nw": op_ld_nw, "ld_x": op_ld_x, "ld_w": op_ld_w, "nwcopy": op_nwcopy,
-            "nwmm": op_nwmm, "R": op_R, "QW": op_QW, "sq": op_sq, "sd": op_sd, "rs": op_rs, "stt": op_stt,
-            "tp": op_tp, "co": op_co, "qh": op_qh, "mm": op_mm, "s2": op_s2, "sr": op_sr, "vcv": op_vcv, "mx": op_mx, "wbc": op_wbc,
-            "rc": op_rc, "sc": op_sc, "vc": op_vc, "st": op_st,
-        }
-        for op in ORDER:
-            ops[op[0]](*op[1:])
+        prep_w(0)
+        for j in range(MT // 2):
+            rs = [stats(2 * j + i) for i in range(2)]
+            for i in range(2):
+                prep_h(2 * j + i, rs[i])
+            out_pair(j, 0)
+        for nb in (3, 1, 2):
+            prep_w(nb)
+            for j in range(MT // 2):
+                out_pair(j, nb)

@@ -43,41 +43,35 @@ def tile_sharedglobalattention_pa_kernel(tc, x, norm_w, Wq, Wk, Wv, out_0, out_1
         nc.vector.memset(nw_row[:], 0.0)
         ones = keep.tile([P, P], BF16, name="ones")
         nc.vector.memset(ones[:], 1.0)
-        ident = keep.tile([P, P], BF16, name="ident")
+        ident = keep.tile([P, P], F32, name="ident")
         make_identity(nc, ident[:])
 
         nw_in = keep.tile([1, D], BF16, name="nw_in")
         nc.sync.dma_start(out=nw_in[:], in_=norm_w.rearrange("(o k) -> o k", o=1))
         x_sb = keep.tile([P, MT, D], BF16, name="x_sb")
         x_view = x.rearrange("b (p m) k -> p (b m) k", m=MT)
-        w_src = [
-            Wq[:, 0:NBW].rearrange("(c p) n -> p c n", p=P),
-            Wq[:, NBW : 2 * NBW].rearrange("(c p) n -> p c n", p=P),
-            Wk.rearrange("(c p) n -> p c n", p=P),
-            Wv.rearrange("(c p) n -> p c n", p=P),
-        ]
-        w_raw = [keep.tile([P, 4 * G, NBW], BF16, name="w_raw%d" % nb) for nb in range(NB)]
+        wq_raw = keep.tile([P, G, 4, 2 * NBW], BF16, name="wq_raw")
+        wk_raw = keep.tile([P, G, 4, NBW], BF16, name="wk_raw")
+        wv_raw = keep.tile([P, G, 4, NBW], BF16, name="wv_raw")
+        w_raw = [wq_raw[:, :, :, 0:NBW], wq_raw[:, :, :, NBW : 2 * NBW], wk_raw[:], wv_raw[:]]
 
         def load_x(m0, m1):
             nc.sync.dma_start(out=x_sb[:, m0:m1, :], in_=x_view[:, m0:m1, :])
 
-        def load_w(nb, g):
-            rows = slice(4 * g, 4 * g + 4)
-            nc.sync.dma_start(out=w_raw[nb][:, rows, :], in_=w_src[nb][:, rows, :])
+        def load_w(dst, src, g):
+            nc.sync.dma_start(out=dst[:, g], in_=src.rearrange("(g p t) n -> p g t n", p=P, t=4)[:, g])
 
-        load_w(0, 0)
+        load_w(wk_raw, Wk, 0)
         load_x(0, 1)
         load_x(1, 2)
-        load_w(0, 1)
+        load_w(wk_raw, Wk, 1)
         load_x(2, 4)
-        load_w(3, 0)
-        load_w(3, 1)
+        load_w(wv_raw, Wv, 0)
+        load_w(wv_raw, Wv, 1)
         load_x(4, 6)
         load_x(6, 8)
-        load_w(1, 0)
-        load_w(1, 1)
-        load_w(2, 0)
-        load_w(2, 1)
+        load_w(wq_raw, Wq, 0)
+        load_w(wq_raw, Wq, 1)
 
         nc.vector.tensor_copy(out=nw_row[0:1, :], in_=nw_in[:])
         wb = psum_w.tile([P, D], BF16, name="wb")
@@ -96,7 +90,7 @@ def tile_sharedglobalattention_pa_kernel(tc, x, norm_w, Wq, Wk, Wv, out_0, out_1
                 wg = work.tile([P, NBW, 4], BF16, name="wg", tag="wg", bufs=4, align_bytes=64)
                 nc.vector.tensor_copy(
                     out=wg[:].rearrange("p (c i) t -> p c t i", i=4),
-                    in_=w_raw[nb][:, 4 * g : 4 * g + 4, :].rearrange("p t (c i) -> p c t i", i=4),
+                    in_=w_raw[nb][:, g].rearrange("p t (c i) -> p c t i", i=4),
                 )
                 grouped.append(wg)
             for g in range(G):
@@ -121,16 +115,17 @@ def tile_sharedglobalattention_pa_kernel(tc, x, norm_w, Wq, Wk, Wv, out_0, out_1
             nc.vector.scalar_tensor_tensor(
                 out=h_sb[:], in0=x_sb[:, m, :], scalar=rstd[:, 0:1], in1=wb[:], op0=ALU.mult, op1=ALU.mult
             )
-            tp = psum.tile([P, 4 * G, P], BF16, name="tp", tag="bank")
-            for c in range(4 * G):
-                nc.tensor.transpose(tp[:, c, :], h_sb[:, c * P : (c + 1) * P], ident[:])
-            hg = work.tile([P, G, P, 4], BF16, name="hg", tag="hg", align_bytes=64)
-            nc.scalar.copy(out=hg[:], in_=tp[:].rearrange("p (g t) r -> p g r t", g=G))
-            nc.vector.quantize_mx(
-                out=h_codes[:, m, :].bitcast(FP8X4),
-                scales=h_scales[:, m, :],
-                in_=hg[:].rearrange("p g r t -> p (g r t)"),
+            words = h_sb[:].bitcast(F32)
+            tp = psum.tile([P, G, 2, P], F32, name="tp", tag="bank")
+            for g in range(G):
+                for u in range(2):
+                    nc.tensor.transpose(tp[:, g, u, :], words[:, 256 * g + u : 256 * (g + 1) : 2], ident[:])
+            hg = work.tile([P, G * P * 4], BF16, name="hg", tag="hg", align_bytes=64)
+            nc.scalar.copy(
+                out=hg[:].bitcast(F32).rearrange("p (g r u) -> p g r u", g=G, u=2),
+                in_=tp[:].rearrange("p g u r -> p g r u"),
             )
+            nc.vector.quantize_mx(out=h_codes[:, m, :].bitcast(FP8X4), scales=h_scales[:, m, :], in_=hg[:])
 
         def project(m, nb):
             acc = psum.tile([P, NBW], F32, name="acc", tag="bank")
@@ -185,13 +180,13 @@ def tile_sharedglobalattention_pa_kernel(tc, x, norm_w, Wq, Wk, Wv, out_0, out_1
                 nc.scalar.copy(out=st[:, :, 1, :], in_=accs[1][:].rearrange("p (h d) -> p h d", h=2))
             nc.sync.dma_start(out=out_views[nb][:, :, 2 * j : 2 * j + 2, :], in_=st[:])
 
-        prep_w(0)
+        prep_w(2)
         for j in range(MT // 2):
             rs = [stats(2 * j + i) for i in range(2)]
             for i in range(2):
                 prep_h(2 * j + i, rs[i])
-            out_pair(j, 0)
-        for nb in (3, 1, 2):
+            out_pair(j, 2)
+        for nb in (3, 0, 1):
             prep_w(nb)
             for j in range(MT // 2):
                 out_pair(j, nb)

@@ -14,15 +14,14 @@ ACT = mybir.ActivationFunctionType
 ALU = mybir.AluOpType
 
 P = 128
-L = 1024
 D = 1024
 HD = 256
-MT = L // P
-NB = 4
+MT = 8
 NBW = 512
 G = 2
 EPS_RMS = 1e-6
 EPS_NORM = 1e-12
+Q01, Q23, KB, VB = range(4)
 
 
 def tile_sharedglobalattention_pa_kernel(tc, x, norm_w, Wq, Wk, Wv, out_0, out_1, out_2):
@@ -32,8 +31,7 @@ def tile_sharedglobalattention_pa_kernel(tc, x, norm_w, Wq, Wk, Wv, out_0, out_1
         stage_pool = ctx.enter_context(tc.tile_pool(name="stage", bufs=1))
         work = ctx.enter_context(tc.tile_pool(name="work", bufs=3))
         small = ctx.enter_context(tc.tile_pool(name="small", bufs=4))
-        psum = ctx.enter_context(tc.psum_pool(name="psum", bufs=7))
-        psum_w = ctx.enter_context(tc.psum_pool(name="psum_w", bufs=1))
+        psum = ctx.enter_context(tc.psum_pool(name="psum", bufs=8))
 
         eps_t = keep.tile([P, 1], F32, name="eps_t")
         nc.vector.memset(eps_t[:], EPS_RMS)
@@ -53,7 +51,7 @@ def tile_sharedglobalattention_pa_kernel(tc, x, norm_w, Wq, Wk, Wv, out_0, out_1
         wq_raw = keep.tile([P, G, 4, 2 * NBW], BF16, name="wq_raw")
         wk_raw = keep.tile([P, G, 4, NBW], BF16, name="wk_raw")
         wv_raw = keep.tile([P, G, 4, NBW], BF16, name="wv_raw")
-        w_raw = [wq_raw[:, :, :, 0:NBW], wq_raw[:, :, :, NBW : 2 * NBW], wk_raw[:], wv_raw[:]]
+        w_raw = {Q01: wq_raw[:, :, :, 0:NBW], Q23: wq_raw[:, :, :, NBW : 2 * NBW], KB: wk_raw[:], VB: wv_raw[:]}
 
         def load_x(m0, m1):
             nc.sync.dma_start(out=x_sb[:, m0:m1, :], in_=x_view[:, m0:m1, :])
@@ -66,66 +64,87 @@ def tile_sharedglobalattention_pa_kernel(tc, x, norm_w, Wq, Wk, Wv, out_0, out_1
         load_x(1, 2)
         load_w(wk_raw, Wk, 1)
         load_x(2, 4)
-        load_w(wv_raw, Wv, 0)
-        load_w(wv_raw, Wv, 1)
         load_x(4, 6)
+        load_w(wv_raw, Wv, 0)
         load_x(6, 8)
+        load_w(wv_raw, Wv, 1)
         load_w(wq_raw, Wq, 0)
         load_w(wq_raw, Wq, 1)
 
         nc.vector.tensor_copy(out=nw_row[0:1, :], in_=nw_in[:])
-        wb = psum_w.tile([P, D], BF16, name="wb")
+        wb = psum.tile([P, D], BF16, name="wb", tag="bank")
         for half in range(2):
             cols = slice(half * 512, (half + 1) * 512)
             nc.tensor.matmul(wb[:, cols], lhsT=ones[:], rhs=nw_row[:, cols], start=True, stop=True)
 
         h_codes = keep.tile([P, MT, G * P], U32, name="h_codes", align_bytes=64)
         h_scales = keep.tile([P, MT, G * P], U8, name="h_scales", align_bytes=64)
-        w_codes = keep.tile([P, NB, G, NBW], U32, name="w_codes", align_bytes=64)
-        w_scales = keep.tile([P, NB, G, NBW], U8, name="w_scales", align_bytes=64)
+        w_codes = keep.tile([P, 4, G, NBW], U32, name="w_codes", align_bytes=64)
+        w_scales = keep.tile([P, 4, G, NBW], U8, name="w_scales", align_bytes=64)
 
-        def prep_w(nb):
-            grouped = []
-            for g in range(G):
-                wg = work.tile([P, NBW, 4], BF16, name="wg", tag="wg", bufs=4, align_bytes=64)
-                nc.vector.tensor_copy(
-                    out=wg[:].rearrange("p (c i) t -> p c t i", i=4),
-                    in_=w_raw[nb][:, g].rearrange("p t (c i) -> p c t i", i=4),
-                )
-                grouped.append(wg)
-            for g in range(G):
-                nc.vector.quantize_mx(
-                    out=w_codes[:, nb, g, :].bitcast(FP8X4),
-                    scales=w_scales[:, nb, g, :],
-                    in_=grouped[g][:].rearrange("p n t -> p (n t)"),
-                )
+        grouped = {}
 
-        def stats(m):
+        def group_w(nb, g):
+            wg = work.tile([P, NBW, 4], BF16, name="wg", tag="wg", bufs=4, align_bytes=64)
+            nc.vector.tensor_copy(
+                out=wg[:].rearrange("p (c i) t -> p c t i", i=4),
+                in_=w_raw[nb][:, g].rearrange("p t (c i) -> p c t i", i=4),
+            )
+            grouped[nb, g] = wg
+
+        def quantize_w(nb, g):
+            nc.vector.quantize_mx(
+                out=w_codes[:, nb, g, :].bitcast(FP8X4),
+                scales=w_scales[:, nb, g, :],
+                in_=grouped[nb, g][:].rearrange("p n t -> p (n t)"),
+            )
+
+        x_ss = keep.tile([P, MT], F32, name="x_ss")
+        x_sd = keep.tile([P, MT], F32, name="x_sd")
+        rstd = keep.tile([P, MT], F32, name="rstd")
+
+        def x_square(m):
             junk = work.tile([P, D], BF16, name="junk", tag="junk", bufs=4)
-            ss = small.tile([P, 1], F32, name="ss", tag="ss")
-            nc.scalar.activation(out=junk[:], in_=x_sb[:, m, :], func=ACT.Square, accum_out=ss[:])
-            sd = small.tile([P, 1], F32, name="sd", tag="sd")
-            nc.scalar.activation(out=sd[:], in_=ss[:], func=ACT.Sqrt, scale=1.0 / D, bias=eps_t[:])
-            rstd = small.tile([P, 1], F32, name="rstd", tag="rstd")
-            nc.vector.reciprocal(out=rstd[:], in_=sd[:])
-            return rstd
+            nc.scalar.activation(out=junk[:], in_=x_sb[:, m, :], func=ACT.Square, accum_out=x_ss[:, m : m + 1])
 
-        def prep_h(m, rstd):
+        def x_root(m):
+            two = slice(m, m + 2)
+            nc.scalar.activation(out=x_sd[:, two], in_=x_ss[:, two], func=ACT.Sqrt, scale=1.0 / D, bias=eps_t[:])
+
+        def x_recip(m):
+            nc.vector.reciprocal(out=rstd[:, m : m + 2], in_=x_sd[:, m : m + 2])
+
+        h_rows = {}
+        h_turned = {}
+        h_grouped = {}
+
+        def normalise(m):
             h_sb = work.tile([P, D], BF16, name="h_sb", tag="h_sb")
             nc.vector.scalar_tensor_tensor(
-                out=h_sb[:], in0=x_sb[:, m, :], scalar=rstd[:, 0:1], in1=wb[:], op0=ALU.mult, op1=ALU.mult
+                out=h_sb[:], in0=x_sb[:, m, :], scalar=rstd[:, m : m + 1], in1=wb[:], op0=ALU.mult, op1=ALU.mult
             )
-            words = h_sb[:].bitcast(F32)
+            h_rows[m] = h_sb
+
+        def turn(m):
+            words = h_rows[m][:].bitcast(F32)
             tp = psum.tile([P, G, 2, P], F32, name="tp", tag="bank")
             for g in range(G):
                 for u in range(2):
                     nc.tensor.transpose(tp[:, g, u, :], words[:, 256 * g + u : 256 * (g + 1) : 2], ident[:])
+            h_turned[m] = tp
+
+        def group_h(m):
             hg = work.tile([P, G * P * 4], BF16, name="hg", tag="hg", align_bytes=64)
             nc.scalar.copy(
                 out=hg[:].bitcast(F32).rearrange("p (g r u) -> p g r u", g=G, u=2),
-                in_=tp[:].rearrange("p g u r -> p g r u"),
+                in_=h_turned[m][:].rearrange("p g u r -> p g r u"),
             )
-            nc.vector.quantize_mx(out=h_codes[:, m, :].bitcast(FP8X4), scales=h_scales[:, m, :], in_=hg[:])
+            h_grouped[m] = hg
+
+        def quantize_h(m):
+            nc.vector.quantize_mx(out=h_codes[:, m, :].bitcast(FP8X4), scales=h_scales[:, m, :], in_=h_grouped[m][:])
+
+        accs = {}
 
         def project(m, nb):
             acc = psum.tile([P, NBW], F32, name="acc", tag="bank")
@@ -139,54 +158,210 @@ def tile_sharedglobalattention_pa_kernel(tc, x, norm_w, Wq, Wk, Wv, out_0, out_1
                     start=(g == 0),
                     stop=(g == G - 1),
                 )
-            return acc
+            accs[m, nb] = acc
 
-        out_views = [
-            out_0.rearrange("b h (p m) d -> p (b h) m d", m=MT)[:, 0:2],
-            out_0.rearrange("b h (p m) d -> p (b h) m d", m=MT)[:, 2:4],
-            out_1.rearrange("b h (p m) d -> p (b h) m d", m=MT),
-            out_2.rearrange("b h (p m) d -> p (b h) m d", m=MT),
-        ]
+        out_q = out_0.rearrange("b h (p m) d -> p (b h) m d", m=MT)
+        out_views = {
+            Q01: out_q[:, 0:2],
+            Q23: out_q[:, 2:4],
+            KB: out_1.rearrange("b h (p m) d -> p (b h) m d", m=MT),
+            VB: out_2.rearrange("b h (p m) d -> p (b h) m d", m=MT),
+        }
+        stages = {}
 
-        def out_pair(j, nb):
-            st = stage_pool.tile([P, 2, 2, HD], F32, name="st_%d_%d" % (nb, j))
-            accs = [project(2 * j + i, nb) for i in range(2)]
-            if nb < 3:
-                ss4 = small.tile([P, 4], F32, name="ss4", tag="ss4")
-                for i in range(2):
-                    for hh in range(2):
-                        jq = work.tile([P, HD], BF16, name="jq", tag="jq", bufs=4)
-                        nc.scalar.activation(
-                            out=jq[:],
-                            in_=accs[i][:, hh * HD : (hh + 1) * HD],
-                            func=ACT.Square,
-                            accum_out=ss4[:, 2 * i + hh : 2 * i + hh + 1],
-                        )
-                nr = small.tile([P, 4], F32, name="nr", tag="nr")
-                nc.scalar.activation(out=nr[:], in_=ss4[:], func=ACT.Sqrt)
-                rn = small.tile([P, 4], F32, name="rn", tag="rn")
-                nc.vector.reciprocal(out=rn[:], in_=nr[:])
-                for i in range(2):
-                    nc.vector.scalar_tensor_tensor(
-                        out=st[:, :, i, :],
-                        in0=rn[:, 2 * i : 2 * i + 2].unsqueeze(2).to_broadcast([P, 2, HD]),
-                        scalar=1.0 / EPS_NORM,
-                        in1=accs[i][:].rearrange("p (h d) -> p h d", h=2),
-                        op0=ALU.min,
-                        op1=ALU.mult,
-                    )
-            else:
-                nc.scalar.copy(out=st[:, :, 0, :], in_=accs[0][:].rearrange("p (h d) -> p h d", h=2))
-                nc.scalar.copy(out=st[:, :, 1, :], in_=accs[1][:].rearrange("p (h d) -> p h d", h=2))
-            nc.sync.dma_start(out=out_views[nb][:, :, 2 * j : 2 * j + 2, :], in_=st[:])
+        def staged(m, nb):
+            if (m // 2, nb) not in stages:
+                stages[m // 2, nb] = stage_pool.tile([P, 2, 2, HD], F32, name="st_%d_%d" % (nb, m // 2))
+            return stages[m // 2, nb][:, :, m % 2, :]
 
-        prep_w(2)
-        for j in range(MT // 2):
-            rs = [stats(2 * j + i) for i in range(2)]
-            for i in range(2):
-                prep_h(2 * j + i, rs[i])
-            out_pair(j, 2)
-        for nb in (3, 0, 1):
-            prep_w(nb)
-            for j in range(MT // 2):
-                out_pair(j, nb)
+        def store(j, nb):
+            nc.sync.dma_start(out=out_views[nb][:, :, 2 * j : 2 * j + 2, :], in_=stages[j, nb][:])
+
+        sums = {}
+        roots = {}
+        recips = {}
+        clipped = {}
+
+        def head_squares(m, nb):
+            j = m // 2
+            if m % 2 == 0:
+                sums[j, nb] = small.tile([P, 4], F32, name="ss4", tag="ss")
+            for hh in range(2):
+                jq = work.tile([P, HD], BF16, name="jq", tag="jq", bufs=4)
+                col = 2 * (m % 2) + hh
+                nc.scalar.activation(
+                    out=jq[:],
+                    in_=accs[m, nb][:, hh * HD : (hh + 1) * HD],
+                    func=ACT.Square,
+                    accum_out=sums[j, nb][:, col : col + 1],
+                )
+
+        def head_roots(j, nb):
+            roots[j, nb] = small.tile([P, 4], F32, name="nr", tag="nr")
+            nc.scalar.activation(out=roots[j, nb][:], in_=sums[j, nb][:], func=ACT.Sqrt)
+
+        def head_recips(j, nb):
+            recips[j, nb] = small.tile([P, 4], F32, name="rn", tag="rn")
+            nc.vector.reciprocal(out=recips[j, nb][:], in_=roots[j, nb][:])
+
+        def clip_recips(j, nb):
+            clipped[j, nb] = small.tile([P, 4], F32, name="rc", tag="rc")
+            nc.vector.tensor_scalar_min(clipped[j, nb][:], recips[j, nb][:], 1.0 / EPS_NORM)
+
+        def scale_vector(m, nb):
+            c0 = 2 * (m % 2)
+            nc.vector.scalar_tensor_tensor(
+                out=staged(m, nb),
+                in0=recips[m // 2, nb][:, c0 : c0 + 2].unsqueeze(2).to_broadcast([P, 2, HD]),
+                scalar=1.0 / EPS_NORM,
+                in1=accs[m, nb][:].rearrange("p (h d) -> p h d", h=2),
+                op0=ALU.min,
+                op1=ALU.mult,
+            )
+
+        def scale_scalar(m, nb):
+            out = staged(m, nb)
+            for hh in range(2):
+                col = 2 * (m % 2) + hh
+                nc.scalar.activation(
+                    out=out[:, hh, :],
+                    in_=accs[m, nb][:, hh * HD : (hh + 1) * HD],
+                    func=ACT.Copy,
+                    scale=clipped[m // 2, nb][:, col : col + 1],
+                )
+
+        def copy_v(m):
+            nc.scalar.copy(out=staged(m, VB), in_=accs[m, VB][:].rearrange("p (h d) -> p h d", h=2))
+
+        with tc.manual_schedule():
+            group_w(KB, 0)
+            x_square(0)
+            x_square(1)
+            group_w(KB, 1)
+            quantize_w(KB, 0)
+            x_square(2)
+            x_root(0)
+            x_square(3)
+            quantize_w(KB, 1)
+            x_square(4)
+            x_root(2)
+            x_recip(0)
+
+            def k_scale(m):
+                scale_scalar(m, KB)
+                if m % 2 == 1:
+                    store(m // 2, KB)
+
+            def k_scale_vector(j):
+                scale_vector(2 * j, KB)
+                scale_vector(2 * j + 1, KB)
+                store(j, KB)
+
+            def v_out(m):
+                project(m, VB)
+                copy_v(m)
+                if m % 2 == 1:
+                    store(m // 2, VB)
+
+            def q_squares(nb, j):
+                for m in (2 * j, 2 * j + 1):
+                    project(m, nb)
+                for m in (2 * j, 2 * j + 1):
+                    head_squares(m, nb)
+
+            def q_scale(nb, j):
+                scale_vector(2 * j, nb)
+                scale_vector(2 * j + 1, nb)
+                store(j, nb)
+
+            def q_scale_both(nb, j):
+                scale_vector(2 * j, nb)
+                scale_scalar(2 * j + 1, nb)
+                store(j, nb)
+
+            for i in range(MT + 3):
+                if 1 <= i <= MT:
+                    group_h(i - 1)
+                if i < MT:
+                    normalise(i)
+                    turn(i)
+                if 2 <= i < MT + 2:
+                    quantize_h(i - 2)
+                    project(i - 2, KB)
+                if i >= 5 and i % 2 == 1 and i - 5 < MT:
+                    head_recips((i - 5) // 2, KB)
+                if 3 <= i < MT + 3:
+                    head_squares(i - 3, KB)
+                if i + 5 < MT:
+                    x_square(i + 5)
+                if i % 2 == 1 and i + 3 < MT:
+                    x_root(i + 3)
+                if i % 2 == 1 and i + 1 < MT:
+                    x_recip(i + 1)
+                if i == 8:
+                    group_w(Q01, 0)
+                if i == 9:
+                    group_w(Q01, 1)
+                if i == 10:
+                    quantize_w(Q01, 0)
+                    quantize_w(Q01, 1)
+                if i >= 5 and i % 2 == 1 and i - 5 < MT:
+                    clip_recips((i - 5) // 2, KB)
+                if i >= 6:
+                    k_scale(i - 6)
+                if i >= 4 and i % 2 == 0 and i - 4 < MT:
+                    head_roots((i - 4) // 2, KB)
+            group_w(VB, 0)
+            head_recips(3, KB)
+            k_scale(5)
+            q_squares(Q01, 0)
+            group_w(VB, 1)
+            q_squares(Q01, 1)
+            head_roots(0, Q01)
+            k_scale_vector(3)
+            quantize_w(VB, 0)
+            head_recips(0, Q01)
+            quantize_w(VB, 1)
+            q_squares(Q01, 2)
+            head_roots(1, Q01)
+            clip_recips(0, Q01)
+            q_scale_both(Q01, 0)
+            v_out(0)
+            v_out(1)
+            group_w(Q23, 0)
+            head_recips(1, Q01)
+            group_w(Q23, 1)
+            clip_recips(1, Q01)
+            quantize_w(Q23, 0)
+            v_out(2)
+            head_roots(2, Q01)
+            q_scale_both(Q01, 1)
+            quantize_w(Q23, 1)
+            q_squares(Q01, 3)
+            head_recips(2, Q01)
+            v_out(3)
+            head_roots(3, Q01)
+            q_scale(Q01, 2)
+            head_recips(3, Q01)
+            q_squares(Q23, 0)
+            v_out(4)
+            head_roots(0, Q23)
+            q_scale(Q01, 3)
+            head_recips(0, Q23)
+            q_squares(Q23, 1)
+            v_out(5)
+            head_roots(1, Q23)
+            q_scale(Q23, 0)
+            q_squares(Q23, 2)
+            head_recips(1, Q23)
+            q_scale(Q23, 1)
+            head_roots(2, Q23)
+            v_out(6)
+            q_squares(Q23, 3)
+            head_recips(2, Q23)
+            q_scale(Q23, 2)
+            head_roots(3, Q23)
+            v_out(7)
+            head_recips(3, Q23)
+            clip_recips(3, Q23)
+            q_scale_both(Q23, 3)

@@ -59,14 +59,15 @@ def tile_sharedglobalattention_pa_kernel(tc, x, norm_w, Wq, Wk, Wv, out_0, out_1
         def load_w(dst, src, g):
             nc.sync.dma_start(out=dst[:, g], in_=src.rearrange("(g p t) n -> p g t n", p=P, t=4)[:, g])
 
-        load_w(wk_raw, Wk, 0)
         load_x(0, 1)
         load_x(1, 2)
+        load_x(2, 3)
+        load_w(wk_raw, Wk, 0)
+        load_x(3, 4)
         load_w(wk_raw, Wk, 1)
-        load_x(2, 4)
         load_x(4, 6)
-        load_w(wv_raw, Wv, 0)
         load_x(6, 8)
+        load_w(wv_raw, Wv, 0)
         load_w(wv_raw, Wv, 1)
         load_w(wq_raw, Wq, 0)
         load_w(wq_raw, Wq, 1)
@@ -92,6 +93,19 @@ def tile_sharedglobalattention_pa_kernel(tc, x, norm_w, Wq, Wk, Wv, out_0, out_1
             )
             grouped[nb, g] = wg
 
+        def group_w_gpsimd(nb, g, part):
+            if part == 0:
+                grouped[nb, g] = work.tile([P, NBW, 4], BF16, name="wg_side", tag="wg_side", bufs=2, align_bytes=64)
+            cols = slice(part * P, (part + 1) * P)
+            nc.gpsimd.tensor_scalar(
+                out=grouped[nb, g][:, cols, :].rearrange("p (c i) t -> p c t i", i=4),
+                in0=w_raw[nb][:, g, :, cols].rearrange("p t (c i) -> p c t i", i=4),
+                scalar1=1.0,
+                scalar2=0.0,
+                op0=ALU.mult,
+                op1=ALU.add,
+            )
+
         def quantize_w(nb, g):
             nc.vector.quantize_mx(
                 out=w_codes[:, nb, g, :].bitcast(FP8X4),
@@ -106,6 +120,18 @@ def tile_sharedglobalattention_pa_kernel(tc, x, norm_w, Wq, Wk, Wv, out_0, out_1
         def x_square(m):
             junk = work.tile([P, D], BF16, name="junk", tag="junk", bufs=4)
             nc.scalar.activation(out=junk[:], in_=x_sb[:, m, :], func=ACT.Square, accum_out=x_ss[:, m : m + 1])
+
+        def x_square_vector(m):
+            junk = work.tile([P, D], BF16, name="junk", tag="junk", bufs=4)
+            nc.vector.scalar_tensor_tensor(
+                out=junk[:],
+                in0=x_sb[:, m, :],
+                scalar=1.0,
+                in1=x_sb[:, m, :],
+                op0=ALU.mult,
+                op1=ALU.mult,
+                accum_out=x_ss[:, m : m + 1],
+            )
 
         def x_root(m):
             two = slice(m, m + 2)
@@ -234,18 +260,27 @@ def tile_sharedglobalattention_pa_kernel(tc, x, norm_w, Wq, Wk, Wv, out_0, out_1
             nc.scalar.copy(out=staged(m, VB), in_=accs[m, VB][:].rearrange("p (h d) -> p h d", h=2))
 
         with tc.manual_schedule():
-            group_w(KB, 0)
-            x_square(0)
+            x_square_vector(0)
             x_square(1)
-            group_w(KB, 1)
-            quantize_w(KB, 0)
-            x_square(2)
             x_root(0)
+            x_square(2)
+            x_recip(0)
+            normalise(0)
+            turn(0)
+            normalise(1)
+            turn(1)
             x_square(3)
-            quantize_w(KB, 1)
+            group_h(0)
             x_square(4)
             x_root(2)
-            x_recip(0)
+            group_h(1)
+            x_square(5)
+            x_root(4)
+            group_w(KB, 0)
+            group_w(KB, 1)
+            quantize_w(KB, 0)
+            x_recip(2)
+            quantize_w(KB, 1)
 
             def k_scale(m):
                 scale_scalar(m, KB)
@@ -256,6 +291,12 @@ def tile_sharedglobalattention_pa_kernel(tc, x, norm_w, Wq, Wk, Wv, out_0, out_1
                 scale_vector(2 * j, KB)
                 scale_vector(2 * j + 1, KB)
                 store(j, KB)
+
+            def v_out_vector(m):
+                project(m, VB)
+                nc.vector.tensor_copy(out=staged(m, VB), in_=accs[m, VB][:].rearrange("p (h d) -> p h d", h=2))
+                if m % 2 == 1:
+                    store(m // 2, VB)
 
             def v_out(m):
                 project(m, VB)
@@ -279,8 +320,17 @@ def tile_sharedglobalattention_pa_kernel(tc, x, norm_w, Wq, Wk, Wv, out_0, out_1
                 scale_scalar(2 * j + 1, nb)
                 store(j, nb)
 
-            for i in range(MT + 3):
-                if 1 <= i <= MT:
+            def store_one(m, nb):
+                nc.sync.dma_start(out=out_views[nb][:, :, m : m + 1, :], in_=stages[m // 2, nb][:, :, m % 2 : m % 2 + 1, :])
+
+            def last_pair(nb, j):
+                scale_vector(2 * j, nb)
+                store_one(2 * j, nb)
+                scale_scalar(2 * j + 1, nb)
+                store_one(2 * j + 1, nb)
+
+            for i in range(2, MT + 3):
+                if 3 <= i < MT:
                     group_h(i - 1)
                 if i < MT:
                     normalise(i)
@@ -292,76 +342,70 @@ def tile_sharedglobalattention_pa_kernel(tc, x, norm_w, Wq, Wk, Wv, out_0, out_1
                     head_recips((i - 5) // 2, KB)
                 if 3 <= i < MT + 3:
                     head_squares(i - 3, KB)
-                if i + 5 < MT:
-                    x_square(i + 5)
-                if i % 2 == 1 and i + 3 < MT:
-                    x_root(i + 3)
+                if i == MT:
+                    group_h(i - 1)
+                if i in (2, 3):
+                    x_square(i + 4)
+                if i == 4:
+                    x_root(6)
+                    for g in range(G):
+                        for part in range(4):
+                            group_w_gpsimd(Q23, g, part)
+                if i == 7:
+                    group_w(VB, 0)
+                if i == 8:
+                    group_w(VB, 1)
+                if i == 9:
+                    quantize_w(VB, 0)
+                if i == 10:
+                    quantize_w(VB, 1)
                 if i % 2 == 1 and i + 1 < MT:
                     x_recip(i + 1)
-                if i == 8:
-                    group_w(Q01, 0)
-                if i == 9:
-                    group_w(Q01, 1)
-                if i == 10:
-                    quantize_w(Q01, 0)
-                    quantize_w(Q01, 1)
                 if i >= 5 and i % 2 == 1 and i - 5 < MT:
                     clip_recips((i - 5) // 2, KB)
                 if i >= 6:
                     k_scale(i - 6)
                 if i >= 4 and i % 2 == 0 and i - 4 < MT:
                     head_roots((i - 4) // 2, KB)
-            group_w(VB, 0)
-            head_recips(3, KB)
             k_scale(5)
-            q_squares(Q01, 0)
-            group_w(VB, 1)
-            q_squares(Q01, 1)
-            head_roots(0, Q01)
+            group_w(Q01, 0)
+            for m in range(6):
+                project(m, VB)
+            for m in range(4):
+                copy_v(m)
+                if m % 2 == 1:
+                    store(m // 2, VB)
+            head_recips(3, KB)
+            group_w(Q01, 1)
             k_scale_vector(3)
-            quantize_w(VB, 0)
-            head_recips(0, Q01)
-            quantize_w(VB, 1)
-            q_squares(Q01, 2)
-            head_roots(1, Q01)
-            clip_recips(0, Q01)
-            q_scale_both(Q01, 0)
-            v_out(0)
-            v_out(1)
-            group_w(Q23, 0)
-            head_recips(1, Q01)
-            group_w(Q23, 1)
-            clip_recips(1, Q01)
+            for m in range(4, 6):
+                copy_v(m)
+            store(2, VB)
+            quantize_w(Q01, 0)
+            quantize_w(Q01, 1)
+            v_out_vector(6)
+            v_out_vector(7)
+            pairs = [(nb, j) for nb in (Q01, Q23) for j in range(MT // 2)]
+            q_squares(Q01, 0)
             quantize_w(Q23, 0)
-            v_out(2)
-            head_roots(2, Q01)
-            q_scale_both(Q01, 1)
             quantize_w(Q23, 1)
-            q_squares(Q01, 3)
-            head_recips(2, Q01)
-            v_out(3)
-            head_roots(3, Q01)
-            q_scale(Q01, 2)
-            head_recips(3, Q01)
-            q_squares(Q23, 0)
-            v_out(4)
-            head_roots(0, Q23)
-            q_scale(Q01, 3)
-            head_recips(0, Q23)
-            q_squares(Q23, 1)
-            v_out(5)
-            head_roots(1, Q23)
-            q_scale(Q23, 0)
-            q_squares(Q23, 2)
-            head_recips(1, Q23)
-            q_scale(Q23, 1)
-            head_roots(2, Q23)
-            v_out(6)
-            q_squares(Q23, 3)
-            head_recips(2, Q23)
-            q_scale(Q23, 2)
+            for n in range(1, len(pairs)):
+                nb, j = pairs[n]
+                last_nb, last_j = pairs[n - 1]
+                for m in (2 * j, 2 * j + 1):
+                    project(m, nb)
+                head_squares(2 * j, nb)
+                head_roots(last_j, last_nb)
+                head_squares(2 * j + 1, nb)
+                head_recips(last_j, last_nb)
+                if n > 1:
+                    scale_vector(2 * pairs[n - 2][1] + 1, pairs[n - 2][0])
+                    store(pairs[n - 2][1], pairs[n - 2][0])
+                scale_vector(2 * last_j, last_nb)
             head_roots(3, Q23)
-            v_out(7)
+            clip_recips(2, Q23)
             head_recips(3, Q23)
+            scale_scalar(5, Q23)
+            store(2, Q23)
             clip_recips(3, Q23)
-            q_scale_both(Q23, 3)
+            last_pair(Q23, 3)

@@ -93,19 +93,6 @@ def tile_sharedglobalattention_pa_kernel(tc, x, norm_w, Wq, Wk, Wv, out_0, out_1
             )
             grouped[nb, g] = wg
 
-        def group_w_gpsimd(nb, g, part):
-            if part == 0:
-                grouped[nb, g] = work.tile([P, NBW, 4], BF16, name="wg_side", tag="wg_side", bufs=2, align_bytes=64)
-            cols = slice(part * P, (part + 1) * P)
-            nc.gpsimd.tensor_scalar(
-                out=grouped[nb, g][:, cols, :].rearrange("p (c i) t -> p c t i", i=4),
-                in0=w_raw[nb][:, g, :, cols].rearrange("p t (c i) -> p c t i", i=4),
-                scalar1=1.0,
-                scalar2=0.0,
-                op0=ALU.mult,
-                op1=ALU.add,
-            )
-
         def quantize_w(nb, g):
             nc.vector.quantize_mx(
                 out=w_codes[:, nb, g, :].bitcast(FP8X4),
@@ -348,9 +335,6 @@ def tile_sharedglobalattention_pa_kernel(tc, x, norm_w, Wq, Wk, Wv, out_0, out_1
                     x_square(i + 4)
                 if i == 4:
                     x_root(6)
-                    for g in range(G):
-                        for part in range(4):
-                            group_w_gpsimd(Q23, g, part)
                 if i == 7:
                     group_w(VB, 0)
                 if i == 8:
@@ -383,12 +367,12 @@ def tile_sharedglobalattention_pa_kernel(tc, x, norm_w, Wq, Wk, Wv, out_0, out_1
             store(2, VB)
             quantize_w(Q01, 0)
             quantize_w(Q01, 1)
-            v_out_vector(6)
-            v_out_vector(7)
             pairs = [(nb, j) for nb in (Q01, Q23) for j in range(MT // 2)]
+            v_out(6)
+            group_w(Q23, 0)
             q_squares(Q01, 0)
-            quantize_w(Q23, 0)
-            quantize_w(Q23, 1)
+            v_out(7)
+            group_w(Q23, 1)
             for n in range(1, len(pairs)):
                 nb, j = pairs[n]
                 last_nb, last_j = pairs[n - 1]
@@ -398,7 +382,14 @@ def tile_sharedglobalattention_pa_kernel(tc, x, norm_w, Wq, Wk, Wv, out_0, out_1
                 head_roots(last_j, last_nb)
                 head_squares(2 * j + 1, nb)
                 head_recips(last_j, last_nb)
-                if n > 1:
+                if n == 1:
+                    quantize_w(Q23, 0)
+                    clip_recips(last_j, last_nb)
+                if n == 2:
+                    quantize_w(Q23, 1)
+                    scale_scalar(1, Q01)
+                    store(0, Q01)
+                elif n > 1:
                     scale_vector(2 * pairs[n - 2][1] + 1, pairs[n - 2][0])
                     store(pairs[n - 2][1], pairs[n - 2][0])
                 scale_vector(2 * last_j, last_nb)

@@ -57,7 +57,10 @@ def tile_sharedglobalattention_pa_kernel(tc, x, norm_w, Wq, Wk, Wv, out_0, out_1
             nc.sync.dma_start(out=x_sb[:, m0:m1, :], in_=x_view[:, m0:m1, :])
 
         def load_w(dst, src, g):
-            nc.sync.dma_start(out=dst[:, g], in_=src.rearrange("(g p t) n -> p g t n", p=P, t=4)[:, g])
+            nc.sync.dma_start(
+                out=dst[:, g].rearrange("p (u e) n -> p u (e n)", u=2),
+                in_=src.rearrange("(g u p e) n -> g p u (e n)", g=G, u=2, e=2)[g],
+            )
 
         load_x(0, 1)
         load_x(1, 2)
@@ -143,7 +146,7 @@ def tile_sharedglobalattention_pa_kernel(tc, x, norm_w, Wq, Wk, Wv, out_0, out_1
             tp = psum.tile([P, G, 2, P], F32, name="tp", tag="bank")
             for g in range(G):
                 for u in range(2):
-                    nc.tensor.transpose(tp[:, g, u, :], words[:, 256 * g + u : 256 * (g + 1) : 2], ident[:])
+                    nc.tensor.transpose(tp[:, g, u, :], words[:, 256 * g + P * u : 256 * g + P * (u + 1)], ident[:])
             h_turned[m] = tp
 
         def group_h(m):

@@ -45,7 +45,6 @@ def tile_sharedglobalattention_pa_kernel(tc, x, norm_w, Wq, Wk, Wv, out_0, out_1
         make_identity(nc, ident[:])
 
         nw_in = keep.tile([1, D], BF16, name="nw_in")
-        nc.sync.dma_start(out=nw_in[:], in_=norm_w.rearrange("(o k) -> o k", o=1))
         x_sb = keep.tile([P, MT, D], BF16, name="x_sb")
         x_view = x.rearrange("b (p m) k -> p (b m) k", m=MT)
         wq_raw = keep.tile([P, G, 4, 2 * NBW], BF16, name="wq_raw")
@@ -63,9 +62,10 @@ def tile_sharedglobalattention_pa_kernel(tc, x, norm_w, Wq, Wk, Wv, out_0, out_1
             )
 
         load_x(0, 1)
+        nc.sync.dma_start(out=nw_in[:], in_=norm_w.rearrange("(o k) -> o k", o=1))
         load_x(1, 2)
-        load_x(2, 3)
         load_w(wk_raw, Wk, 0)
+        load_x(2, 3)
         load_x(3, 4)
         load_w(wk_raw, Wk, 1)
         load_x(4, 6)
@@ -75,7 +75,7 @@ def tile_sharedglobalattention_pa_kernel(tc, x, norm_w, Wq, Wk, Wv, out_0, out_1
         load_w(wq_raw, Wq, 0)
         load_w(wq_raw, Wq, 1)
 
-        nc.vector.tensor_copy(out=nw_row[0:1, :], in_=nw_in[:])
+        nc.scalar.copy(out=nw_row[0:1, :], in_=nw_in[:])
         wb = psum.tile([P, D], BF16, name="wb", tag="bank")
         for half in range(2):
             cols = slice(half * 512, (half + 1) * 512)
@@ -95,6 +95,19 @@ def tile_sharedglobalattention_pa_kernel(tc, x, norm_w, Wq, Wk, Wv, out_0, out_1
                 in_=w_raw[nb][:, g].rearrange("p t (c i) -> p c t i", i=4),
             )
             grouped[nb, g] = wg
+
+        def group_w_gpsimd(nb, g, part):
+            if part == 0:
+                grouped[nb, g] = work.tile([P, NBW, 4], BF16, name="wg_side", tag="wg_side", bufs=2, align_bytes=64)
+            cols = slice(part * (NBW // 8), (part + 1) * (NBW // 8))
+            nc.gpsimd.tensor_scalar(
+                out=grouped[nb, g][:, cols, :].rearrange("p (c i) t -> p c t i", i=4),
+                in0=w_raw[nb][:, g, :, cols].rearrange("p t (c i) -> p c t i", i=4),
+                scalar1=1.0,
+                scalar2=0.0,
+                op0=ALU.mult,
+                op1=ALU.add,
+            )
 
         def quantize_w(nb, g):
             nc.vector.quantize_mx(
@@ -254,19 +267,19 @@ def tile_sharedglobalattention_pa_kernel(tc, x, norm_w, Wq, Wk, Wv, out_0, out_1
             x_square(1)
             x_root(0)
             x_square(2)
+            group_w(KB, 0)
             x_recip(0)
             normalise(0)
             turn(0)
             normalise(1)
             turn(1)
             x_square(3)
+            x_root(2)
             group_h(0)
             x_square(4)
-            x_root(2)
             group_h(1)
             x_square(5)
             x_root(4)
-            group_w(KB, 0)
             group_w(KB, 1)
             quantize_w(KB, 0)
             x_recip(2)
@@ -338,6 +351,9 @@ def tile_sharedglobalattention_pa_kernel(tc, x, norm_w, Wq, Wk, Wv, out_0, out_1
                     x_square(i + 4)
                 if i == 4:
                     x_root(6)
+                    for g in range(G):
+                        for part in range(8):
+                            group_w_gpsimd(Q01, g, part)
                 if i == 7:
                     group_w(VB, 0)
                 if i == 8:
@@ -350,56 +366,57 @@ def tile_sharedglobalattention_pa_kernel(tc, x, norm_w, Wq, Wk, Wv, out_0, out_1
                     x_recip(i + 1)
                 if i >= 5 and i % 2 == 1 and i - 5 < MT:
                     clip_recips((i - 5) // 2, KB)
-                if i >= 6:
+                if 6 <= i < 10:
                     k_scale(i - 6)
                 if i >= 4 and i % 2 == 0 and i - 4 < MT:
                     head_roots((i - 4) // 2, KB)
-            k_scale(5)
-            group_w(Q01, 0)
-            for m in range(6):
-                project(m, VB)
+            quantize_w(Q01, 0)
+            quantize_w(Q01, 1)
             for m in range(4):
+                project(m, VB)
                 copy_v(m)
                 if m % 2 == 1:
                     store(m // 2, VB)
+            k_scale_vector(2)
             head_recips(3, KB)
-            group_w(Q01, 1)
             k_scale_vector(3)
-            for m in range(4, 6):
-                copy_v(m)
-            store(2, VB)
-            quantize_w(Q01, 0)
-            quantize_w(Q01, 1)
+            v_out(4)
+            v_out(5)
             pairs = [(nb, j) for nb in (Q01, Q23) for j in range(MT // 2)]
-            v_out(6)
             group_w(Q23, 0)
             q_squares(Q01, 0)
+            v_out(6)
+            head_roots(0, Q01)
             v_out(7)
             group_w(Q23, 1)
+            head_recips(0, Q01)
             for n in range(1, len(pairs)):
                 nb, j = pairs[n]
                 last_nb, last_j = pairs[n - 1]
                 for m in (2 * j, 2 * j + 1):
                     project(m, nb)
                 head_squares(2 * j, nb)
-                head_roots(last_j, last_nb)
+                if n > 1:
+                    head_roots(last_j, last_nb)
                 head_squares(2 * j + 1, nb)
-                head_recips(last_j, last_nb)
                 if n == 1:
                     quantize_w(Q23, 0)
-                    clip_recips(last_j, last_nb)
-                if n == 2:
-                    quantize_w(Q23, 1)
-                    scale_scalar(1, Q01)
-                    store(0, Q01)
-                elif n > 1:
+                    scale_vector(0, Q01)
+                if n > 1:
+                    if n > 3:
+                        head_recips(last_j, last_nb)
                     scale_vector(2 * pairs[n - 2][1] + 1, pairs[n - 2][0])
                     store(pairs[n - 2][1], pairs[n - 2][0])
-                scale_vector(2 * last_j, last_nb)
+                    if n <= 3:
+                        head_recips(last_j, last_nb)
+                    if n == 2:
+                        quantize_w(Q23, 1)
+                    if n == 7:
+                        clip_recips(2, Q23)
+                    scale_vector(2 * last_j, last_nb)
             head_roots(3, Q23)
-            clip_recips(2, Q23)
-            head_recips(3, Q23)
             scale_scalar(5, Q23)
             store(2, Q23)
+            head_recips(3, Q23)
             clip_recips(3, Q23)
             last_pair(Q23, 3)

@@ -67,19 +67,13 @@ def tile_sharedglobalattention_pa_kernel(tc, x, norm_w, Wq, Wk, Wv, out_0, out_1
         load_w(wk_raw, Wk, 0)
         load_x(2, 3)
         load_x(3, 4)
-        load_w(wk_raw, Wk, 1)
         load_x(4, 6)
+        load_w(wk_raw, Wk, 1)
         load_x(6, 8)
         load_w(wv_raw, Wv, 0)
         load_w(wv_raw, Wv, 1)
         load_w(wq_raw, Wq, 0)
         load_w(wq_raw, Wq, 1)
-
-        nc.scalar.copy(out=nw_row[0:1, :], in_=nw_in[:])
-        wb = psum.tile([P, D], BF16, name="wb", tag="bank")
-        for half in range(2):
-            cols = slice(half * 512, (half + 1) * 512)
-            nc.tensor.matmul(wb[:, cols], lhsT=ones[:], rhs=nw_row[:, cols], start=True, stop=True)
 
         h_codes = keep.tile([P, MT, G * P], U32, name="h_codes", align_bytes=64)
         h_scales = keep.tile([P, MT, G * P], U8, name="h_scales", align_bytes=64)
@@ -87,6 +81,15 @@ def tile_sharedglobalattention_pa_kernel(tc, x, norm_w, Wq, Wk, Wv, out_0, out_1
         w_scales = keep.tile([P, 4, G, NBW], U8, name="w_scales", align_bytes=64)
 
         grouped = {}
+
+        def group_w_half(nb, g, half):
+            if half == 0:
+                grouped[nb, g] = work.tile([P, NBW, 4], BF16, name="wg", tag="wg", bufs=4, align_bytes=64)
+            cols = slice(half * (NBW // 2), (half + 1) * (NBW // 2))
+            nc.vector.tensor_copy(
+                out=grouped[nb, g][:, cols, :].rearrange("p (c i) t -> p c t i", i=4),
+                in_=w_raw[nb][:, g, :, cols].rearrange("p t (c i) -> p c t i", i=4),
+            )
 
         def group_w(nb, g):
             wg = work.tile([P, NBW, 4], BF16, name="wg", tag="wg", bufs=4, align_bytes=64)
@@ -98,7 +101,7 @@ def tile_sharedglobalattention_pa_kernel(tc, x, norm_w, Wq, Wk, Wv, out_0, out_1
 
         def group_w_gpsimd(nb, g, part):
             if part == 0:
-                grouped[nb, g] = work.tile([P, NBW, 4], BF16, name="wg_side", tag="wg_side", bufs=2, align_bytes=64)
+                grouped[nb, g] = work.tile([P, NBW, 4], BF16, name="wg_side", tag="wg_side", bufs=3, align_bytes=64)
             cols = slice(part * (NBW // 8), (part + 1) * (NBW // 8))
             nc.gpsimd.tensor_scalar(
                 out=grouped[nb, g][:, cols, :].rearrange("p (c i) t -> p c t i", i=4),
@@ -266,24 +269,32 @@ def tile_sharedglobalattention_pa_kernel(tc, x, norm_w, Wq, Wk, Wv, out_0, out_1
             x_square_vector(0)
             x_square(1)
             x_root(0)
+            nc.vector.tensor_copy(out=nw_row[0:1, :], in_=nw_in[:])
+            wb = psum.tile([P, D], BF16, name="wb", tag="bank")
+            for half in range(2):
+                cols = slice(half * 512, (half + 1) * 512)
+                nc.tensor.matmul(wb[:, cols], lhsT=ones[:], rhs=nw_row[:, cols], start=True, stop=True)
             x_square(2)
-            group_w(KB, 0)
+            group_w_half(KB, 0, 0)
             x_recip(0)
+            group_w_half(KB, 0, 1)
             normalise(0)
             turn(0)
             normalise(1)
             turn(1)
             x_square(3)
             x_root(2)
-            group_h(0)
             x_square(4)
-            group_h(1)
+            group_h(0)
             x_square(5)
+            group_h(1)
             x_root(4)
             group_w(KB, 1)
             quantize_w(KB, 0)
             x_recip(2)
             quantize_w(KB, 1)
+            for part in range(8):
+                group_w_gpsimd(VB, 0, part)
 
             def k_scale(m):
                 scale_scalar(m, KB)
@@ -355,8 +366,6 @@ def tile_sharedglobalattention_pa_kernel(tc, x, norm_w, Wq, Wk, Wv, out_0, out_1
                         for part in range(8):
                             group_w_gpsimd(Q01, g, part)
                 if i == 7:
-                    group_w(VB, 0)
-                if i == 8:
                     group_w(VB, 1)
                 if i == 9:
                     quantize_w(VB, 0)

@@ -112,6 +112,13 @@ def tile_sharedglobalattention_pa_kernel(tc, x, norm_w, Wq, Wk, Wv, out_0, out_1
                 op1=ALU.add,
             )
 
+        def group_rest(nb, g, part):
+            cols = slice(part * (NBW // 8), NBW)
+            nc.vector.tensor_copy(
+                out=grouped[nb, g][:, cols, :].rearrange("p (c i) t -> p c t i", i=4),
+                in_=w_raw[nb][:, g, :, cols].rearrange("p t (c i) -> p c t i", i=4),
+            )
+
         def quantize_w(nb, g):
             nc.vector.quantize_mx(
                 out=w_codes[:, nb, g, :].bitcast(FP8X4),
@@ -282,6 +289,9 @@ def tile_sharedglobalattention_pa_kernel(tc, x, norm_w, Wq, Wk, Wv, out_0, out_1
             turn(0)
             normalise(1)
             turn(1)
+            busy = psum.tile([P, NBW], F32, name="busy", tag="bank")
+            for repeat in range(5):
+                nc.tensor.matmul(busy[:], lhsT=ones[:], rhs=nw_row[:, 0:NBW], start=True, stop=True)
             x_square(3)
             x_root(2)
             x_square(4)
@@ -362,9 +372,10 @@ def tile_sharedglobalattention_pa_kernel(tc, x, norm_w, Wq, Wk, Wv, out_0, out_1
                     x_square(i + 4)
                 if i == 4:
                     x_root(6)
-                    for g in range(G):
-                        for part in range(8):
-                            group_w_gpsimd(Q01, g, part)
+                    for part in range(8):
+                        group_w_gpsimd(Q01, 0, part)
+                    for part in range(6):
+                        group_w_gpsimd(Q01, 1, part)
                 if i == 7:
                     group_w(VB, 1)
                 if i == 9:
@@ -379,6 +390,7 @@ def tile_sharedglobalattention_pa_kernel(tc, x, norm_w, Wq, Wk, Wv, out_0, out_1
                     k_scale(i - 6)
                 if i >= 4 and i % 2 == 0 and i - 4 < MT:
                     head_roots((i - 4) // 2, KB)
+            group_rest(Q01, 1, 6)
             quantize_w(Q01, 0)
             quantize_w(Q01, 1)
             for m in range(4):

@@ -221,7 +221,7 @@ def tile_sharedglobalattention_pa_kernel(tc, x, norm_w, Wq, Wk, Wv, out_0, out_1
         recips = {}
         clipped = {}
 
-        def head_squares(m, nb):
+        def head_squares(m, nb, before=None):
             j = m // 2
             if m % 2 == 0:
                 sums[j, nb] = small.tile([P, 4], F32, name="ss4", tag="ss")
@@ -234,6 +234,8 @@ def tile_sharedglobalattention_pa_kernel(tc, x, norm_w, Wq, Wk, Wv, out_0, out_1
                     func=ACT.Square,
                     accum_out=sums[j, nb][:, col : col + 1],
                 )
+                if hh == 0 and before is not None:
+                    head_roots(*before)
 
         def head_roots(j, nb):
             roots[j, nb] = small.tile([P, 4], F32, name="nr", tag="nr")
@@ -416,9 +418,7 @@ def tile_sharedglobalattention_pa_kernel(tc, x, norm_w, Wq, Wk, Wv, out_0, out_1
                 last_nb, last_j = pairs[n - 1]
                 for m in (2 * j, 2 * j + 1):
                     project(m, nb)
-                head_squares(2 * j, nb)
-                if n > 1:
-                    head_roots(last_j, last_nb)
+                head_squares(2 * j, nb, (last_j, last_nb) if n > 1 else None)
                 head_squares(2 * j + 1, nb)
                 if n == 1:
                     quantize_w(Q23, 0)

from contextlib import ExitStack

import concourse.mybir as mybir
from concourse.masks import make_identity

FLOPS = 2 * 1024 * 1024 * 2048

BF16 = mybir.dt.bfloat16
F32 = mybir.dt.float32
U32 = mybir.dt.uint32
U8 = mybir.dt.uint8
FP8X4 = mybir.dt.float8_e4m3fn_x4
ACT = mybir.ActivationFunctionType
ALU = mybir.AluOpType

P = 128
D = 1024
HD = 256
MT = 8
NBW = 512
G = 2
EPS_RMS = 1e-6
EPS_NORM = 1e-12
Q01, Q23, KB, VB = range(4)


def tile_sharedglobalattention_pa_kernel(tc, x, norm_w, Wq, Wk, Wv, out_0, out_1, out_2):
    nc = tc.nc
    with ExitStack() as ctx:
        keep = ctx.enter_context(tc.tile_pool(name="keep", bufs=1))
        stage_pool = ctx.enter_context(tc.tile_pool(name="stage", bufs=1))
        work = ctx.enter_context(tc.tile_pool(name="work", bufs=3))
        small = ctx.enter_context(tc.tile_pool(name="small", bufs=4))
        psum = ctx.enter_context(tc.psum_pool(name="psum", bufs=8))

        eps_t = keep.tile([P, 1], F32, name="eps_t")
        nc.vector.memset(eps_t[:], EPS_RMS)
        warm = keep.tile([P, 1], F32, name="warm")
        nc.scalar.activation(out=warm[:], in_=eps_t[:], func=ACT.Sqrt)
        nw_row = keep.tile([P, D], BF16, name="nw_row")
        nc.vector.memset(nw_row[:], 0.0)
        ones = keep.tile([P, P], BF16, name="ones")
        nc.vector.memset(ones[:], 1.0)
        ident = keep.tile([P, P], F32, name="ident")
        make_identity(nc, ident[:])

        nw_in = keep.tile([1, D], BF16, name="nw_in")
        x_sb = keep.tile([P, MT, D], BF16, name="x_sb")
        x_view = x.rearrange("b (p m) k -> p (b m) k", m=MT)
        wq_raw = keep.tile([P, G, 4, 2 * NBW], BF16, name="wq_raw")
        wk_raw = keep.tile([P, G, 4, NBW], BF16, name="wk_raw")
        wv_raw = keep.tile([P, G, 4, NBW], BF16, name="wv_raw")
        w_raw = {Q01: wq_raw[:, :, :, 0:NBW], Q23: wq_raw[:, :, :, NBW : 2 * NBW], KB: wk_raw[:], VB: wv_raw[:]}

        def load_x(m0, m1):
            nc.sync.dma_start(out=x_sb[:, m0:m1, :], in_=x_view[:, m0:m1, :])

        def load_w(dst, src, g):
            nc.sync.dma_start(
                out=dst[:, g].rearrange("p (u e) n -> p u (e n)", u=2),
                in_=src.rearrange("(g u p e) n -> g p u (e n)", g=G, u=2, e=2)[g],
            )

        load_x(0, 1)
        nc.sync.dma_start(out=nw_in[:], in_=norm_w.rearrange("(o k) -> o k", o=1))
        load_x(1, 2)
        load_w(wk_raw, Wk, 0)
        load_x(2, 3)
        load_x(3, 4)
        load_x(4, 6)
        load_w(wk_raw, Wk, 1)
        load_x(6, 8)
        load_w(wv_raw, Wv, 0)
        load_w(wv_raw, Wv, 1)
        load_w(wq_raw, Wq, 0)
        load_w(wq_raw, Wq, 1)

        h_codes = keep.tile([P, MT, G * P], U32, name="h_codes", align_bytes=64)
        h_scales = keep.tile([P, MT, G * P], U8, name="h_scales", align_bytes=64)
        w_codes = keep.tile([P, 4, G, NBW], U32, name="w_codes", align_bytes=64)
        w_scales = keep.tile([P, 4, G, NBW], U8, name="w_scales", align_bytes=64)

        grouped = {}

        def group_w_half(nb, g, half):
            if half == 0:
                grouped[nb, g] = work.tile([P, NBW, 4], BF16, name="wg", tag="wg", bufs=4, align_bytes=64)
            cols = slice(half * (NBW // 2), (half + 1) * (NBW // 2))
            nc.vector.tensor_copy(
                out=grouped[nb, g][:, cols, :].rearrange("p (c i) t -> p c t i", i=4),
                in_=w_raw[nb][:, g, :, cols].rearrange("p t (c i) -> p c t i", i=4),
            )

        def group_w(nb, g):
            wg = work.tile([P, NBW, 4], BF16, name="wg", tag="wg", bufs=4, align_bytes=64)
            nc.vector.tensor_copy(
                out=wg[:].rearrange("p (c i) t -> p c t i", i=4),
                in_=w_raw[nb][:, g].rearrange("p t (c i) -> p c t i", i=4),
            )
            grouped[nb, g] = wg

        def group_w_gpsimd(nb, g, part):
            if part == 0:
                grouped[nb, g] = work.tile([P, NBW, 4], BF16, name="wg_side", tag="wg_side", bufs=3, align_bytes=64)
            cols = slice(part * (NBW // 8), (part + 1) * (NBW // 8))
            nc.gpsimd.tensor_scalar(
                out=grouped[nb, g][:, cols, :].rearrange("p (c i) t -> p c t i", i=4),
                in0=w_raw[nb][:, g, :, cols].rearrange("p t (c i) -> p c t i", i=4),
                scalar1=1.0,
                scalar2=0.0,
                op0=ALU.mult,
                op1=ALU.add,
            )

        def group_rest(nb, g, part):
            cols = slice(part * (NBW // 8), NBW)
            nc.vector.tensor_copy(
                out=grouped[nb, g][:, cols, :].rearrange("p (c i) t -> p c t i", i=4),
                in_=w_raw[nb][:, g, :, cols].rearrange("p t (c i) -> p c t i", i=4),
            )

        def quantize_w(nb, g):
            nc.vector.quantize_mx(
                out=w_codes[:, nb, g, :].bitcast(FP8X4),
                scales=w_scales[:, nb, g, :],
                in_=grouped[nb, g][:].rearrange("p n t -> p (n t)"),
            )

        x_ss = keep.tile([P, MT], F32, name="x_ss")
        x_sd = keep.tile([P, MT], F32, name="x_sd")
        rstd = keep.tile([P, MT], F32, name="rstd")

        def x_square(m):
            junk = work.tile([P, D], BF16, name="junk", tag="junk", bufs=4)
            nc.scalar.activation(out=junk[:], in_=x_sb[:, m, :], func=ACT.Square, accum_out=x_ss[:, m : m + 1])

        def x_square_vector(m):
            junk = work.tile([P, D], BF16, name="junk", tag="junk", bufs=4)
            nc.vector.scalar_tensor_tensor(
                out=junk[:],
                in0=x_sb[:, m, :],
                scalar=1.0,
                in1=x_sb[:, m, :],
                op0=ALU.mult,
                op1=ALU.mult,
                accum_out=x_ss[:, m : m + 1],
            )

        def x_root(m):
            two = slice(m, m + 2)
            nc.scalar.activation(out=x_sd[:, two], in_=x_ss[:, two], func=ACT.Sqrt, scale=1.0 / D, bias=eps_t[:])

        def x_recip(m):
            nc.vector.reciprocal(out=rstd[:, m : m + 2], in_=x_sd[:, m : m + 2])

        h_rows = {}
        h_turned = {}
        h_grouped = {}

        def normalise(m):
            h_sb = work.tile([P, D], BF16, name="h_sb", tag="h_sb")
            nc.vector.scalar_tensor_tensor(
                out=h_sb[:], in0=x_sb[:, m, :], scalar=rstd[:, m : m + 1], in1=wb[:], op0=ALU.mult, op1=ALU.mult
            )
            h_rows[m] = h_sb

        def turn(m):
            words = h_rows[m][:].bitcast(F32)
            tp = psum.tile([P, G, 2, P], F32, name="tp", tag="bank")
            for g in range(G):
                for u in range(2):
                    nc.tensor.transpose(tp[:, g, u, :], words[:, 256 * g + P * u : 256 * g + P * (u + 1)], ident[:])
            h_turned[m] = tp

        def group_h(m):
            hg = work.tile([P, G * P * 4], BF16, name="hg", tag="hg", align_bytes=64)
            nc.scalar.copy(
                out=hg[:].bitcast(F32).rearrange("p (g r u) -> p g r u", g=G, u=2),
                in_=h_turned[m][:].rearrange("p g u r -> p g r u"),
            )
            h_grouped[m] = hg

        def quantize_h(m):
            nc.vector.quantize_mx(out=h_codes[:, m, :].bitcast(FP8X4), scales=h_scales[:, m, :], in_=h_grouped[m][:])

        accs = {}

        def project(m, nb):
            acc = psum.tile([P, NBW], F32, name="acc", tag="bank")
            for g in range(G):
                nc.tensor.matmul_mx(
                    out=acc[:],
                    lhsT=h_codes[:, m, g * P : (g + 1) * P].bitcast(FP8X4),
                    lhsT_scale=h_scales[:, m, g * P : (g + 1) * P],
                    rhs=w_codes[:, nb, g, :].bitcast(FP8X4),
                    rhs_scale=w_scales[:, nb, g, :],
                    start=(g == 0),
                    stop=(g == G - 1),
                )
            accs[m, nb] = acc

        out_q = out_0.rearrange("b h (p m) d -> p (b h) m d", m=MT)
        out_views = {
            Q01: out_q[:, 0:2],
            Q23: out_q[:, 2:4],
            KB: out_1.rearrange("b h (p m) d -> p (b h) m d", m=MT),
            VB: out_2.rearrange("b h (p m) d -> p (b h) m d", m=MT),
        }
        stages = {}

        def staged(m, nb):
            if (m // 2, nb) not in stages:
                stages[m // 2, nb] = stage_pool.tile([P, 2, 2, HD], F32, name="st_%d_%d" % (nb, m // 2))
            return stages[m // 2, nb][:, :, m % 2, :]

        def store(j, nb):
            nc.sync.dma_start(out=out_views[nb][:, :, 2 * j : 2 * j + 2, :], in_=stages[j, nb][:])

        sums = {}
        roots = {}
        recips = {}
        clipped = {}

        def head_squares(m, nb, before=None):
            j = m // 2
            if m % 2 == 0:
                sums[j, nb] = small.tile([P, 4], F32, name="ss4", tag="ss")
            for hh in range(2):
                jq = work.tile([P, HD], BF16, name="jq", tag="jq", bufs=4)
                col = 2 * (m % 2) + hh
                nc.scalar.activation(
                    out=jq[:],
                    in_=accs[m, nb][:, hh * HD : (hh + 1) * HD],
                    func=ACT.Square,
                    accum_out=sums[j, nb][:, col : col + 1],
                )
                if hh == 0 and before is not None:
                    head_roots(*before)

        def head_roots(j, nb):
            roots[j, nb] = small.tile([P, 4], F32, name="nr", tag="nr")
            nc.scalar.activation(out=roots[j, nb][:], in_=sums[j, nb][:], func=ACT.Sqrt)

        def head_recips(j, nb):
            recips[j, nb] = small.tile([P, 4], F32, name="rn", tag="rn")
            nc.vector.reciprocal(out=recips[j, nb][:], in_=roots[j, nb][:])

        def clip_recips(j, nb):
            clipped[j, nb] = small.tile([P, 4], F32, name="rc", tag="rc")
            nc.vector.tensor_scalar_min(clipped[j, nb][:], recips[j, nb][:], 1.0 / EPS_NORM)

        def scale_vector(m, nb):
            c0 = 2 * (m % 2)
            nc.vector.scalar_tensor_tensor(
                out=staged(m, nb),
                in0=recips[m // 2, nb][:, c0 : c0 + 2].unsqueeze(2).to_broadcast([P, 2, HD]),
                scalar=1.0 / EPS_NORM,
                in1=accs[m, nb][:].rearrange("p (h d) -> p h d", h=2),
                op0=ALU.min,
                op1=ALU.mult,
            )

        def scale_scalar(m, nb):
            out = staged(m, nb)
            for hh in range(2):
                col = 2 * (m % 2) + hh
                nc.scalar.activation(
                    out=out[:, hh, :],
                    in_=accs[m, nb][:, hh * HD : (hh + 1) * HD],
                    func=ACT.Copy,
                    scale=clipped[m // 2, nb][:, col : col + 1],
                )

        def copy_v(m):
            nc.scalar.copy(out=staged(m, VB), in_=accs[m, VB][:].rearrange("p (h d) -> p h d", h=2))

        with tc.manual_schedule():
            x_square_vector(0)
            x_square(1)
            x_root(0)
            nc.vector.tensor_copy(out=nw_row[0:1, :], in_=nw_in[:])
            wb = psum.tile([P, D], BF16, name="wb", tag="bank")
            for half in range(2):
                cols = slice(half * 512, (half + 1) * 512)
                nc.tensor.matmul(wb[:, cols], lhsT=ones[:], rhs=nw_row[:, cols], start=True, stop=True)
            x_square(2)
            group_w_half(KB, 0, 0)
            x_recip(0)
            group_w_half(KB, 0, 1)
            normalise(0)
            turn(0)
            normalise(1)
            turn(1)
            busy = psum.tile([P, NBW], F32, name="busy", tag="bank")
            for repeat in range(5):
                nc.tensor.matmul(busy[:], lhsT=ones[:], rhs=nw_row[:, 0:NBW], start=True, stop=True)
            x_square(3)
            x_root(2)
            x_square(4)
            group_h(0)
            x_square(5)
            group_h(1)
            x_root(4)
            group_w(KB, 1)
            quantize_w(KB, 0)
            x_recip(2)
            quantize_w(KB, 1)
            for part in range(8):
                group_w_gpsimd(VB, 0, part)

            def k_scale(m):
                scale_scalar(m, KB)
                if m % 2 == 1:
                    store(m // 2, KB)

            def k_scale_vector(j):
                scale_vector(2 * j, KB)
                scale_vector(2 * j + 1, KB)
                store(j, KB)

            def v_out_vector(m):
                project(m, VB)
                nc.vector.tensor_copy(out=staged(m, VB), in_=accs[m, VB][:].rearrange("p (h d) -> p h d", h=2))
                if m % 2 == 1:
                    store(m // 2, VB)

            def v_out(m):
                project(m, VB)
                copy_v(m)
                if m % 2 == 1:
                    store(m // 2, VB)

            def q_squares(nb, j):
                for m in (2 * j, 2 * j + 1):
                    project(m, nb)
                for m in (2 * j, 2 * j + 1):
                    head_squares(m, nb)

            def q_scale(nb, j):
                scale_vector(2 * j, nb)
                scale_vector(2 * j + 1, nb)
                store(j, nb)

            def q_scale_both(nb, j):
                scale_vector(2 * j, nb)
                scale_scalar(2 * j + 1, nb)
                store(j, nb)

            def store_one(m, nb):
                nc.sync.dma_start(out=out_views[nb][:, :, m : m + 1, :], in_=stages[m // 2, nb][:, :, m % 2 : m % 2 + 1, :])

            def last_pair(nb, j):
                scale_vector(2 * j, nb)
                store_one(2 * j, nb)
                scale_scalar(2 * j + 1, nb)
                store_one(2 * j + 1, nb)

            for i in range(2, MT + 3):
                if 3 <= i < MT:
                    group_h(i - 1)
                if i < MT:
                    normalise(i)
                    turn(i)
                if 2 <= i < MT + 2:
                    quantize_h(i - 2)
                    project(i - 2, KB)
                if i >= 5 and i % 2 == 1 and i - 5 < MT:
                    head_recips((i - 5) // 2, KB)
                if 3 <= i < MT + 3:
                    head_squares(i - 3, KB)
                if i == MT:
                    group_h(i - 1)
                if i in (2, 3):
                    x_square(i + 4)
                if i == 4:
                    x_root(6)
                    for part in range(8):
                        group_w_gpsimd(Q01, 0, part)
                    for part in range(6):
                        group_w_gpsimd(Q01, 1, part)
                if i == 7:
                    group_w(VB, 1)
                if i == 9:
                    quantize_w(VB, 0)
                if i == 10:
                    quantize_w(VB, 1)
                if i % 2 == 1 and i + 1 < MT:
                    x_recip(i + 1)
                if i >= 5 and i % 2 == 1 and i - 5 < MT:
                    clip_recips((i - 5) // 2, KB)
                if 6 <= i < 10:
                    k_scale(i - 6)
                if i >= 4 and i % 2 == 0 and i - 4 < MT:
                    head_roots((i - 4) // 2, KB)
            group_rest(Q01, 1, 6)
            quantize_w(Q01, 0)
            quantize_w(Q01, 1)
            for m in range(4):
                project(m, VB)
                copy_v(m)
                if m % 2 == 1:
                    store(m // 2, VB)
            k_scale_vector(2)
            head_recips(3, KB)
            k_scale_vector(3)
            v_out(4)
            v_out(5)
            pairs = [(nb, j) for nb in (Q01, Q23) for j in range(MT // 2)]
            group_w(Q23, 0)
            q_squares(Q01, 0)
            v_out(6)
            head_roots(0, Q01)
            v_out(7)
            group_w(Q23, 1)
            head_recips(0, Q01)
            for n in range(1, len(pairs)):
                nb, j = pairs[n]
                last_nb, last_j = pairs[n - 1]
                for m in (2 * j, 2 * j + 1):
                    project(m, nb)
                head_squares(2 * j, nb, (last_j, last_nb) if n > 1 else None)
                head_squares(2 * j + 1, nb)
                if n == 1:
                    quantize_w(Q23, 0)
                    scale_vector(0, Q01)
                if n > 1:
                    if n > 3:
                        head_recips(last_j, last_nb)
                    scale_vector(2 * pairs[n - 2][1] + 1, pairs[n - 2][0])
                    store(pairs[n - 2][1], pairs[n - 2][0])
                    if n <= 3:
                        head_recips(last_j, last_nb)
                    if n == 2:
                        quantize_w(Q23, 1)
                    if n == 7:
                        clip_recips(2, Q23)
                    scale_vector(2 * last_j, last_nb)
            head_roots(3, Q23)
            scale_scalar(5, Q23)
            store(2, Q23)
            head_recips(3, Q23)
            clip_recips(3, Q23)
            last_pair(Q23, 3)
